import numpy as np
import ml_dtypes


def mxq(x, axis, fmt="e4m3"):
    dtype, down = {"e4m3": (ml_dtypes.float8_e4m3fn, 7), "e5m2": (ml_dtypes.float8_e5m2, 14)}[fmt]
    v = np.moveaxis(np.asarray(x, np.float32).astype(ml_dtypes.bfloat16).astype(np.float64), axis, -1)
    blocks = v.reshape(v.shape[:-1] + (-1, 32))
    amax = np.abs(blocks).max(-1, keepdims=True)
    byte = np.maximum(np.where(amax > 0, np.frexp(amax)[1] - 1 + 127, 0) - down, 1)
    scale = np.exp2(byte - 127.0)
    codes = (blocks / scale).astype(np.float32).astype(dtype).astype(np.float64)
    return np.moveaxis((codes * scale).reshape(v.shape), -1, axis)


WIDE = False


def mx_kscale(k):
    if not WIDE:
        return np.ones(k)
    levels = np.array([30, -30])
    if k % 512:
        return np.exp2(np.random.permutation(np.resize(levels, k // 32))).repeat(32)
    a = np.empty((k // 512, 16))
    for p in range(k // 512):
        a[p, :8] = np.random.permutation(np.resize(levels, 8))
        for g in range(8):
            far = levels[np.abs(levels - a[p, g]) >= 10]
            a[p, g + 8] = far[np.random.randint(len(far))]
    return np.exp2(a.ravel()).repeat(32)


BF16 = ml_dtypes.bfloat16


def bf(x):
    return np.asarray(x, np.float32).astype(BF16)


def f64(x):
    return np.asarray(x).astype(np.float64)


B, NF, GH, GW, DX, DIM, NH, CHUNK, SINK, MAXF = 1, 8, 16, 16, 1024, 1024, 8, 2, 1, 4
L = NF * GH * GW
HD = DIM // NH
C = HD // 2
DS = C // 3
DT = C - 2 * DS
MT = max(NF, GH, GW)
EPS = 1e-6


def rope_tables():
    def tab(d):
        inv = 1.0 / (10000.0 ** (np.arange(d) / d))
        ang = np.outer(np.arange(MT), inv)
        return np.cos(ang), np.sin(ang)
    ct, st = tab(DT)
    ch, sh = tab(DS)
    cw, sw = tab(DS)
    return np.concatenate([ct, ch, cw], axis=1), np.concatenate([st, sh, sw], axis=1)


def pos_table(tab):
    t = np.broadcast_to(tab[:NF, :DT][:, None, None, :], (NF, GH, GW, DT))
    hh = np.broadcast_to(tab[:GH, DT:DT + DS][None, :, None, :], (NF, GH, GW, DS))
    ww = np.broadcast_to(tab[:GW, DT + DS:][None, None, :, :], (NF, GH, GW, DS))
    return np.concatenate([t, hh, ww], axis=-1).reshape(L, C)


def setup_inputs():
    s = mx_kscale(DX)
    fc, fs = rope_tables()
    return {"x": bf(np.random.standard_normal((B, L, DX)) * s),
            "W": bf(np.random.standard_normal((DIM, DX)) / np.sqrt(DX) / s[None, :]),
            "b": bf(np.random.standard_normal(DIM) * 0.3),
            "g": bf(1.0 + 0.1 * np.random.standard_normal(DIM)),
            "freqs_cos": bf(fc), "freqs_sin": bf(fs)}


def reference(x, W, b, g, freqs_cos, freqs_sin):
    y = (mxq(f64(x), 2, "e5m2") @ mxq(f64(W), 1, "e5m2").T) + f64(b)
    z = y * (1.0 / np.sqrt(np.mean(y * y, axis=-1, keepdims=True) + EPS)) * f64(g)
    co = pos_table(f64(freqs_cos))[None, :, None, :]
    si = pos_table(f64(freqs_sin))[None, :, None, :]
    a = z.reshape(B, L, NH, C, 2)
    xr, xi = a[..., 0], a[..., 1]
    return np.stack([xr * co - xi * si, xr * si + xi * co], axis=-1).reshape(B, L, NH, HD)

@@ -1,0 +1,282 @@
+from contextlib import ExitStack
+
+import concourse.mybir as mybir
+from concourse.masks import make_identity
+
+FLOPS = 2 * 2048 * 1024 * 1024
+
+F32 = mybir.dt.float32
+BF16 = mybir.dt.bfloat16
+U32 = mybir.dt.uint32
+U8 = mybir.dt.uint8
+FP8X4 = mybir.dt.float8_e5m2_x4
+ACT = mybir.ActivationFunctionType
+ALU = mybir.AluOpType
+
+P = 128
+K = 1024
+NH = 8
+NCH = 4
+EPS = 1e-6
+DT2 = 44
+DRC = 84
+
+
+def tile_causalwanselfattention_pa_kernel(tc, x, W, b, g, freqs_cos, freqs_sin, out):
+    nc = tc.nc
+    x_rows = x.rearrange("o l k -> (o l) k")
+    out_rows = out.rearrange("o l h d -> (o l) (h d)")
+
+    with ExitStack() as ctx:
+        const = ctx.enter_context(tc.tile_pool(name="const", bufs=1))
+        rawp = ctx.enter_context(tc.tile_pool(name="rawp", bufs=24))
+        grp = ctx.enter_context(tc.tile_pool(name="grp", bufs=2))
+        ypool = ctx.enter_context(tc.tile_pool(name="ypool", bufs=2))
+        work = ctx.enter_context(tc.tile_pool(name="work", bufs=3))
+        small = ctx.enter_context(tc.tile_pool(name="small", bufs=4))
+        psum = ctx.enter_context(tc.psum_pool(name="psum", bufs=2))
+
+        src = const.tile([P, 1600], BF16, name="src")
+        nc.vector.memset(src[:], 0.0)
+        nc.scalar.dma_start(out=src[0:16, 0:21], in_=freqs_cos[:, 22:43])
+        nc.scalar.dma_start(out=src[16:32, 21:42], in_=freqs_cos[:, 43:64])
+        nc.scalar.dma_start(out=src[0:16, 48:69], in_=freqs_sin[:, 22:43])
+        nc.scalar.dma_start(out=src[16:32, 69:90], in_=freqs_sin[:, 43:64])
+        nc.scalar.dma_start(
+            out=src[32:33, 96:272].rearrange("o (f j) -> o f j", j=22), in_=freqs_cos[0:8, 0:22].unsqueeze(0)
+        )
+        nc.scalar.dma_start(
+            out=src[32:33, 272:448].rearrange("o (f j) -> o f j", j=22), in_=freqs_sin[0:8, 0:22].unsqueeze(0)
+        )
+        nc.scalar.dma_start(out=src[32:33, 448:1472], in_=g.unsqueeze(0))
+        nc.scalar.dma_start(out=src[64:72, 1472:1600], in_=b.rearrange("(h d) -> h d", d=P))
+
+        raw_tiles = {}
+
+        def load(key, rows):
+            t = rawp.tile([P, K], BF16, tag="raw", name="raw_" + key)
+            nc.sync.dma_start(out=t[:], in_=rows)
+            raw_tiles[key] = t
+
+        for t in range(4):
+            load("x%d" % t, x_rows[P * t : P * (t + 1), :])
+        for h in range(NH):
+            load("w%d" % h, W[P * h : P * (h + 1), :])
+        for t in range(4, 16):
+            load("x%d" % t, x_rows[P * t : P * (t + 1), :])
+
+        ident_f = const.tile([P, P], F32, name="ident_f")
+        make_identity(nc, ident_f[:])
+        ident_b = const.tile([P, P], BF16, name="ident_b")
+        make_identity(nc, ident_b[:])
+
+        wc = const.tile([P, NH, 2, P], U32, name="wc", align_bytes=64)
+        ws = const.tile([P, NH, 2, P], U8, name="ws", align_bytes=64)
+        xc = const.tile([P, NCH, 2, 512], U32, name="xc", align_bytes=64)
+        xs = const.tile([P, NCH, 2, 512], U8, name="xs", align_bytes=64)
+
+        def in_transposes(key):
+            words = raw_tiles[key].bitcast(F32)
+            xt = psum.tile([P, 2, 2, P], F32, tag="xt", name="xt")
+            for gi in range(2):
+                for u in range(2):
+                    nc.tensor.transpose(xt[:, gi, u, :], words[:, 256 * gi + u : 256 * (gi + 1) : 2], ident_f[:])
+            return xt
+
+        def copy_words(on_vector, dst_words, xt):
+            srcv = xt.rearrange("p g u r -> p g r u")
+            if on_vector:
+                nc.vector.tensor_copy(out=dst_words, in_=srcv)
+            else:
+                nc.scalar.copy(out=dst_words, in_=srcv)
+
+        xg_tiles = {}
+
+        def x_tile_in(t, on_vector):
+            c, tt = divmod(t, 4)
+            if tt == 0:
+                xg_tiles[c] = grp.tile([P, 2, 2048], BF16, tag="xg", name="xg", align_bytes=64)
+            xt = in_transposes("x%d" % t)
+            dst = xg_tiles[c].bitcast(F32)[:, :, 256 * tt : 256 * (tt + 1)].rearrange("p g (r u) -> p g r u", u=2)
+            copy_words(on_vector, dst, xt)
+
+        def x_quant(c):
+            for gi in range(2):
+                nc.vector.quantize_mx(
+                    out=xc[:, c, gi, :].bitcast(FP8X4), scales=xs[:, c, gi, :], in_=xg_tiles[c][:, gi, :]
+                )
+
+        wg_tiles = {}
+
+        def w_tile_in(h, on_vector):
+            wg_tiles[h] = grp.tile([P, 2, 512], BF16, tag="wg", name="wg", align_bytes=64, bufs=3)
+            xt = in_transposes("w%d" % h)
+            dst = wg_tiles[h].bitcast(F32).rearrange("p g (r u) -> p g r u", u=2)
+            copy_words(on_vector, dst, xt)
+
+        def w_quant(h):
+            nc.vector.quantize_mx(
+                out=wc[:, h].rearrange("p g m -> p (g m)").bitcast(FP8X4),
+                scales=ws[:, h].rearrange("p g m -> p (g m)"),
+                in_=wg_tiles[h].rearrange("p g n -> p (g n)"),
+            )
+
+        for t in range(4):
+            x_tile_in(t, t % 2 == 0)
+        x_quant(0)
+
+        srce = const.tile([P, 896], BF16, name="srce")
+        srce3 = srce.rearrange("p (n e) -> p n e", e=2)
+        nc.vector.tensor_copy(out=srce3, in_=src[:, 0:448].unsqueeze(2).to_broadcast([P, 448, 2]))
+        nc.vector.tensor_scalar_mul(out=srce3[:, 48:96, 1:2], in0=srce3[:, 48:96, 1:2], scalar1=-1.0)
+        nc.vector.tensor_scalar_mul(out=srce3[:, 272:448, 1:2], in0=srce3[:, 272:448, 1:2], scalar1=-1.0)
+        sel = const.tile([P, 2, P], BF16, name="sel")
+        for par in range(2):
+            nc.vector.tensor_tensor(
+                out=sel[:, par, :].rearrange("p (a c) -> p a c", c=16),
+                in0=ident_b[:, 8 * par : 8 * par + 8].unsqueeze(2).to_broadcast([P, 8, 16]),
+                in1=ident_b[:, 16:32].unsqueeze(1).to_broadcast([P, 8, 16]),
+                op=ALU.add,
+            )
+        row32 = ident_b[:, 32:33].to_broadcast([P, P])
+
+        g_b = const.tile([P, K], F32, name="g_b")
+        pos_t = const.tile([P, 2, 8, DT2], F32, name="pos_t")
+        pos_rc = const.tile([P, 2, 2, DRC], F32, name="pos_rc")
+        b_col = const.tile([P, NH], F32, name="b_col")
+
+        ps_a = psum.tile([P, 512], F32, tag="yT0", name="ps_a")
+        nc.tensor.matmul(out=ps_a[:], lhsT=row32, rhs=src[:, 448:960], start=True, stop=True)
+        nc.scalar.copy(out=g_b[:, 0:512], in_=ps_a[:])
+        ps_b = psum.tile([P, 512], F32, tag="yT1", name="ps_b")
+        nc.tensor.matmul(out=ps_b[:], lhsT=row32, rhs=src[:, 960:1472], start=True, stop=True)
+        nc.scalar.copy(out=g_b[:, 512:1024], in_=ps_b[:])
+        ps_c = psum.tile([P, 512], F32, tag="yT0", name="ps_c")
+        nc.tensor.matmul(out=ps_c[:, 0:352], lhsT=row32, rhs=srce[:, 192:544], start=True, stop=True)
+        nc.scalar.copy(out=pos_t[:, 0].rearrange("p f d -> p (f d)"), in_=ps_c[:, 0:352])
+        ps_d = psum.tile([P, 512], F32, tag="yT1", name="ps_d")
+        nc.tensor.matmul(out=ps_d[:, 0:352], lhsT=row32, rhs=srce[:, 544:896], start=True, stop=True)
+        nc.scalar.copy(out=pos_t[:, 1].rearrange("p f d -> p (f d)"), in_=ps_d[:, 0:352])
+        ps_e = psum.tile([P, 512], F32, tag="acc", name="ps_e")
+        for par in range(2):
+            nc.tensor.matmul(
+                out=ps_e[:, 192 * par : 192 * (par + 1)], lhsT=sel[:, par, :], rhs=srce[:, 0:192], start=True, stop=True
+            )
+        nc.tensor.matmul(out=ps_e[:, 384:392], lhsT=src[:, 1472:1600], rhs=ident_b[:, 64:72], start=True, stop=True)
+        nc.scalar.copy(
+            out=pos_rc[:], in_=ps_e[:, 0:384].rearrange("p (a c n) -> p a c n", a=2, c=2)[:, :, :, 0:DRC]
+        )
+        nc.scalar.copy(out=b_col[:], in_=ps_e[:, 384:392])
+
+        g_b3 = g_b.rearrange("p (h d) -> p h d", d=P)
+        tab_t = const.tile([P, 8, 2, NH, DT2], F32, name="tab_t")
+        tab_rc = const.tile([P, 2, 2, NH, DRC], F32, name="tab_rc")
+
+        def build_tab_t(f):
+            nc.gpsimd.tensor_tensor(
+                out=tab_t[:, f],
+                in0=g_b3[:, :, 0:DT2].unsqueeze(1).to_broadcast([P, 2, NH, DT2]),
+                in1=pos_t[:, :, f, :].unsqueeze(2).to_broadcast([P, 2, NH, DT2]),
+                op=ALU.mult,
+            )
+
+        def build_tab_rc(par):
+            nc.gpsimd.tensor_tensor(
+                out=tab_rc[:, par],
+                in0=g_b3[:, :, DT2:P].unsqueeze(1).to_broadcast([P, 2, NH, DRC]),
+                in1=pos_rc[:, par].unsqueeze(2).to_broadcast([P, 2, NH, DRC]),
+                op=ALU.mult,
+            )
+
+        build_tab_t(0)
+        build_tab_rc(0)
+        build_tab_rc(1)
+        for f in range(1, 8):
+            build_tab_t(f)
+
+        ysb_tiles = {}
+
+        def mx_head(c, h):
+            if h == 0:
+                ysb_tiles[c] = ypool.tile([P, NH, 512], F32, tag="ysb", name="ysb")
+            acc = psum.tile([P, 512], F32, tag="acc", name="acc")
+            for gi in range(2):
+                nc.tensor.matmul_mx(
+                    out=acc[:],
+                    lhsT=wc[:, h, gi, :].bitcast(FP8X4),
+                    lhsT_scale=ws[:, h, gi, :],
+                    rhs=xc[:, c, gi, :].bitcast(FP8X4),
+                    rhs_scale=xs[:, c, gi, :],
+                    start=(gi == 0),
+                    stop=(gi == 1),
+                )
+            nc.scalar.activation(
+                out=ysb_tiles[c][:, h, :], in_=acc[:], func=ACT.Identity, bias=b_col[:, h : h + 1], scale=1.0
+            )
+
+        for h in range(NH):
+            w_tile_in(h, h % 2 == 0)
+            w_quant(h)
+            mx_head(0, h)
+        for t in range(4, 8):
+            x_tile_in(t, t % 2 == 0)
+        x_quant(1)
+
+        def back_transposes(c, tt):
+            banks = []
+            for bk in range(2):
+                yt = psum.tile([P, 512], F32, tag="yT%d" % bk, name="yT%d" % bk)
+                for hh in range(4):
+                    nc.tensor.transpose(
+                        yt[:, P * hh : P * (hh + 1)], ysb_tiles[c][:, 4 * bk + hh, P * tt : P * (tt + 1)], ident_f[:]
+                    )
+                banks.append(yt)
+            return banks
+
+        def epilogue(c, tt, banks):
+            t = 4 * c + tt
+            f, par = divmod(t, 2)
+            ss = small.tile([P, 4], F32, tag="ss", name="ss")
+            for bk in range(2):
+                junk = work.tile([P, 512], F32, tag="junk", name="junk", bufs=2)
+                nc.scalar.activation(
+                    out=junk[:], in_=banks[bk][:], func=ACT.Square, scale=0.03125, accum_out=ss[:, bk : bk + 1]
+                )
+            nc.scalar.activation(out=ss[:, 2:3], in_=ss[:, 1:2], func=ACT.Identity, bias=EPS, scale=1.0)
+            nc.scalar.activation(out=ss[:, 3:4], in_=ss[:, 0:1], func=ACT.Sqrt, bias=ss[:, 2:3], scale=1.0)
+            rstd = small.tile([P, 1], F32, tag="rstd", name="rstd")
+            nc.vector.reciprocal(out=rstd[:], in_=ss[:, 3:4])
+            t1 = work.tile([P, NH, P], F32, tag="t1", name="t1")
+            t2 = work.tile([P, NH, P], F32, tag="t2", name="t2")
+            for bk in range(2):
+                y3 = banks[bk].rearrange("p (h d) -> p h d", d=P)
+                hs = slice(4 * bk, 4 * bk + 4)
+                for cs, dst in ((0, t1), (1, t2)):
+                    nc.vector.scalar_tensor_tensor(
+                        out=dst[:, hs, 0:DT2], in0=y3[:, :, 0:DT2], scalar=rstd[:, 0:1],
+                        in1=tab_t[:, f, cs, hs, :], op0=ALU.mult, op1=ALU.mult,
+                    )
+                    nc.vector.scalar_tensor_tensor(
+                        out=dst[:, hs, DT2:P], in0=y3[:, :, DT2:P], scalar=rstd[:, 0:1],
+                        in1=tab_rc[:, par, cs, hs, :], op0=ALU.mult, op1=ALU.mult,
+                    )
+            o = work.tile([P, K], F32, tag="o", name="o")
+            nc.gpsimd.tensor_tensor(
+                out=o.rearrange("p (n e) -> p n e", e=2),
+                in0=t1.rearrange("p h (j e) -> p (h j) e", e=2),
+                in1=t2.rearrange("p h (j e) -> p (h j) e", e=2)[:, :, ::-1],
+                op=ALU.add,
+            )
+            nc.sync.dma_start(out=out_rows[P * t : P * (t + 1), :], in_=o[:])
+
+        for c in range(NCH):
+            for tt in range(4):
+                banks = back_transposes(c, tt)
+                if c + 1 < NCH:
+                    mx_head(c + 1, 2 * tt)
+                    mx_head(c + 1, 2 * tt + 1)
+                if c + 2 < NCH:
+                    x_tile_in(4 * (c + 2) + tt, tt % 2 == 0)
+                    if tt == 3:
+                        x_quant(c + 2)
+                epilogue(c, tt, banks)

@@ -20,6 +20,10 @@ NCH = 4
 EPS = 1e-6
 DT2 = 44
 DRC = 84
+MANUAL = False
+RC_ON_V = True
+TABS_HEAD = 8
+V_COPIES = ()
 
 
 def tile_causalwanselfattention_pa_kernel(tc, x, W, b, g, freqs_cos, freqs_sin, out):
@@ -32,24 +36,22 @@ def tile_causalwanselfattention_pa_kernel(tc, x, W, b, g, freqs_cos, freqs_sin, 
         rawp = ctx.enter_context(tc.tile_pool(name="rawp", bufs=24))
         grp = ctx.enter_context(tc.tile_pool(name="grp", bufs=2))
         ypool = ctx.enter_context(tc.tile_pool(name="ypool", bufs=2))
-        work = ctx.enter_context(tc.tile_pool(name="work", bufs=3))
+        work = ctx.enter_context(tc.tile_pool(name="work", bufs=4))
         small = ctx.enter_context(tc.tile_pool(name="small", bufs=4))
-        psum = ctx.enter_context(tc.psum_pool(name="psum", bufs=2))
+        psum = ctx.enter_context(tc.psum_pool(name="psum", bufs=1))
+        if MANUAL:
+            ctx.enter_context(tc.manual_schedule())
 
-        src = const.tile([P, 1600], BF16, name="src")
-        nc.vector.memset(src[:], 0.0)
-        nc.scalar.dma_start(out=src[0:16, 0:21], in_=freqs_cos[:, 22:43])
-        nc.scalar.dma_start(out=src[16:32, 21:42], in_=freqs_cos[:, 43:64])
-        nc.scalar.dma_start(out=src[0:16, 48:69], in_=freqs_sin[:, 22:43])
-        nc.scalar.dma_start(out=src[16:32, 69:90], in_=freqs_sin[:, 43:64])
-        nc.scalar.dma_start(
-            out=src[32:33, 96:272].rearrange("o (f j) -> o f j", j=22), in_=freqs_cos[0:8, 0:22].unsqueeze(0)
-        )
-        nc.scalar.dma_start(
-            out=src[32:33, 272:448].rearrange("o (f j) -> o f j", j=22), in_=freqs_sin[0:8, 0:22].unsqueeze(0)
-        )
-        nc.scalar.dma_start(out=src[32:33, 448:1472], in_=g.unsqueeze(0))
-        nc.scalar.dma_start(out=src[64:72, 1472:1600], in_=b.rearrange("(h d) -> h d", d=P))
+        fsrc = const.tile([P, 384], BF16, name="fsrc")
+        nc.vector.memset(fsrc[:], 0.0)
+        warm = const.tile([P, 2], F32, name="warm")
+        nc.vector.memset(warm[:], 1.0)
+        ones_b = const.tile([P, P], BF16, name="ones_b")
+        nc.vector.memset(ones_b[:], 1.0)
+        nc.scalar.dma_start(out=fsrc[0:16, 0:64], in_=freqs_cos)
+        nc.scalar.dma_start(out=fsrc[0:16, 64:128], in_=freqs_sin)
+        nc.sync.dma_start(out=fsrc[0:8, 256:384], in_=g.rearrange("(h d) -> h d", d=P))
+        nc.sync.dma_start(out=fsrc[0:8, 128:256], in_=b.rearrange("(h d) -> h d", d=P))
 
         raw_tiles = {}
 
@@ -65,112 +67,126 @@ def tile_causalwanselfattention_pa_kernel(tc, x, W, b, g, freqs_cos, freqs_sin, 
         for t in range(4, 16):
             load("x%d" % t, x_rows[P * t : P * (t + 1), :])
 
-        ident_f = const.tile([P, P], F32, name="ident_f")
-        make_identity(nc, ident_f[:])
         ident_b = const.tile([P, P], BF16, name="ident_b")
         make_identity(nc, ident_b[:])
+        ident_f = const.tile([P, P], F32, name="ident_f")
+        make_identity(nc, ident_f[:])
+        nc.scalar.activation(out=warm[:, 1:2], in_=warm[:, 0:1], func=ACT.Abs_reciprocal_sqrt)
 
         wc = const.tile([P, NH, 2, P], U32, name="wc", align_bytes=64)
         ws = const.tile([P, NH, 2, P], U8, name="ws", align_bytes=64)
         xc = const.tile([P, NCH, 2, 512], U32, name="xc", align_bytes=64)
         xs = const.tile([P, NCH, 2, 512], U8, name="xs", align_bytes=64)
 
-        def in_transposes(key):
+        xt_of = {}
+        xg_tiles = {}
+        wg_tiles = {}
+
+        def t_in(key, tag):
             words = raw_tiles[key].bitcast(F32)
-            xt = psum.tile([P, 2, 2, P], F32, tag="xt", name="xt")
+            xt = psum.tile([P, 2, 2, P], F32, tag=tag, name="xt_" + key)
             for gi in range(2):
                 for u in range(2):
                     nc.tensor.transpose(xt[:, gi, u, :], words[:, 256 * gi + u : 256 * (gi + 1) : 2], ident_f[:])
-            return xt
+            xt_of[key] = xt
 
-        def copy_words(on_vector, dst_words, xt):
-            srcv = xt.rearrange("p g u r -> p g r u")
-            if on_vector:
-                nc.vector.tensor_copy(out=dst_words, in_=srcv)
+        def c_in(key):
+            n = int(key[1:])
+            if key[0] == "x":
+                c, tt = divmod(n, 4)
+                if tt == 0:
+                    xg_tiles[c] = grp.tile([P, 2, 2048], BF16, tag="xg", name="xg", align_bytes=64)
+                dst = xg_tiles[c].bitcast(F32)[:, :, 256 * tt : 256 * (tt + 1)]
             else:
-                nc.scalar.copy(out=dst_words, in_=srcv)
+                wg_tiles[n] = grp.tile([P, 2, 512], BF16, tag="wg", name="wg", align_bytes=64, bufs=4)
+                dst = wg_tiles[n].bitcast(F32)
+            dst = dst.rearrange("p g (r u) -> p g r u", u=2)
+            srcv = xt_of[key].rearrange("p g u r -> p g r u")
+            if key in V_COPIES:
+                nc.vector.tensor_copy(out=dst, in_=srcv)
+            else:
+                nc.scalar.copy(out=dst, in_=srcv)
 
-        xg_tiles = {}
+        def tc_in(key, tag):
+            t_in(key, tag)
+            c_in(key)
 
-        def x_tile_in(t, on_vector):
-            c, tt = divmod(t, 4)
-            if tt == 0:
-                xg_tiles[c] = grp.tile([P, 2, 2048], BF16, tag="xg", name="xg", align_bytes=64)
-            xt = in_transposes("x%d" % t)
-            dst = xg_tiles[c].bitcast(F32)[:, :, 256 * tt : 256 * (tt + 1)].rearrange("p g (r u) -> p g r u", u=2)
-            copy_words(on_vector, dst, xt)
-
-        def x_quant(c):
+        def q_x(c):
             for gi in range(2):
                 nc.vector.quantize_mx(
                     out=xc[:, c, gi, :].bitcast(FP8X4), scales=xs[:, c, gi, :], in_=xg_tiles[c][:, gi, :]
                 )
 
-        wg_tiles = {}
-
-        def w_tile_in(h, on_vector):
-            wg_tiles[h] = grp.tile([P, 2, 512], BF16, tag="wg", name="wg", align_bytes=64, bufs=3)
-            xt = in_transposes("w%d" % h)
-            dst = wg_tiles[h].bitcast(F32).rearrange("p g (r u) -> p g r u", u=2)
-            copy_words(on_vector, dst, xt)
-
-        def w_quant(h):
+        def q_w(h):
             nc.vector.quantize_mx(
                 out=wc[:, h].rearrange("p g m -> p (g m)").bitcast(FP8X4),
                 scales=ws[:, h].rearrange("p g m -> p (g m)"),
                 in_=wg_tiles[h].rearrange("p g n -> p (g n)"),
             )
 
-        for t in range(4):
-            x_tile_in(t, t % 2 == 0)
-        x_quant(0)
-
-        srce = const.tile([P, 896], BF16, name="srce")
-        srce3 = srce.rearrange("p (n e) -> p n e", e=2)
-        nc.vector.tensor_copy(out=srce3, in_=src[:, 0:448].unsqueeze(2).to_broadcast([P, 448, 2]))
-        nc.vector.tensor_scalar_mul(out=srce3[:, 48:96, 1:2], in0=srce3[:, 48:96, 1:2], scalar1=-1.0)
-        nc.vector.tensor_scalar_mul(out=srce3[:, 272:448, 1:2], in0=srce3[:, 272:448, 1:2], scalar1=-1.0)
-        sel = const.tile([P, 2, P], BF16, name="sel")
-        for par in range(2):
-            nc.vector.tensor_tensor(
-                out=sel[:, par, :].rearrange("p (a c) -> p a c", c=16),
-                in0=ident_b[:, 8 * par : 8 * par + 8].unsqueeze(2).to_broadcast([P, 8, 16]),
-                in1=ident_b[:, 16:32].unsqueeze(1).to_broadcast([P, 8, 16]),
-                op=ALU.add,
-            )
-        row32 = ident_b[:, 32:33].to_broadcast([P, P])
-
         g_b = const.tile([P, K], F32, name="g_b")
         pos_t = const.tile([P, 2, 8, DT2], F32, name="pos_t")
         pos_rc = const.tile([P, 2, 2, DRC], F32, name="pos_rc")
         b_col = const.tile([P, NH], F32, name="b_col")
-
-        ps_a = psum.tile([P, 512], F32, tag="yT0", name="ps_a")
-        nc.tensor.matmul(out=ps_a[:], lhsT=row32, rhs=src[:, 448:960], start=True, stop=True)
-        nc.scalar.copy(out=g_b[:, 0:512], in_=ps_a[:])
-        ps_b = psum.tile([P, 512], F32, tag="yT1", name="ps_b")
-        nc.tensor.matmul(out=ps_b[:], lhsT=row32, rhs=src[:, 960:1472], start=True, stop=True)
-        nc.scalar.copy(out=g_b[:, 512:1024], in_=ps_b[:])
-        ps_c = psum.tile([P, 512], F32, tag="yT0", name="ps_c")
-        nc.tensor.matmul(out=ps_c[:, 0:352], lhsT=row32, rhs=srce[:, 192:544], start=True, stop=True)
-        nc.scalar.copy(out=pos_t[:, 0].rearrange("p f d -> p (f d)"), in_=ps_c[:, 0:352])
-        ps_d = psum.tile([P, 512], F32, tag="yT1", name="ps_d")
-        nc.tensor.matmul(out=ps_d[:, 0:352], lhsT=row32, rhs=srce[:, 544:896], start=True, stop=True)
-        nc.scalar.copy(out=pos_t[:, 1].rearrange("p f d -> p (f d)"), in_=ps_d[:, 0:352])
-        ps_e = psum.tile([P, 512], F32, tag="acc", name="ps_e")
-        for par in range(2):
-            nc.tensor.matmul(
-                out=ps_e[:, 192 * par : 192 * (par + 1)], lhsT=sel[:, par, :], rhs=srce[:, 0:192], start=True, stop=True
-            )
-        nc.tensor.matmul(out=ps_e[:, 384:392], lhsT=src[:, 1472:1600], rhs=ident_b[:, 64:72], start=True, stop=True)
-        nc.scalar.copy(
-            out=pos_rc[:], in_=ps_e[:, 0:384].rearrange("p (a c n) -> p a c n", a=2, c=2)[:, :, :, 0:DRC]
-        )
-        nc.scalar.copy(out=b_col[:], in_=ps_e[:, 384:392])
-
+        fe = const.tile([P, 2, P], BF16, name="fe")
+        x_t = const.tile([P, 2, 8, DT2], BF16, name="x_t")
+        selr = const.tile([P, 2, P], BF16, name="selr")
+        selc = const.tile([P, P], BF16, name="selc")
         g_b3 = g_b.rearrange("p (h d) -> p h d", d=P)
         tab_t = const.tile([P, 8, 2, NH, DT2], F32, name="tab_t")
         tab_rc = const.tile([P, 2, 2, NH, DRC], F32, name="tab_rc")
+
+        def setup_gain_bias():
+            for half, tag in ((0, "A0"), (1, "A1")):
+                ps_g = psum.tile([P, 512], F32, tag=tag, name="ps_g")
+                for hh in range(4):
+                    h = 4 * half + hh
+                    nc.tensor.matmul(
+                        out=ps_g[:, P * hh : P * (hh + 1)], lhsT=ident_b[:, h : h + 1].to_broadcast([P, P]),
+                        rhs=fsrc[:, 256:384], start=True, stop=True,
+                    )
+                nc.scalar.copy(out=g_b[:, 512 * half : 512 * (half + 1)], in_=ps_g[:])
+
+        def setup_vector():
+            nc.vector.tensor_copy(
+                out=fe.rearrange("p c (j e) -> p (c j) e", e=2), in_=fsrc[:, 0:128].unsqueeze(2).to_broadcast([P, P, 2])
+            )
+            sin_odd = fe.rearrange("p c (j e) -> p c j e", e=2)[:, 1, :, 1:2]
+            nc.vector.tensor_scalar_mul(out=sin_odd, in0=sin_odd, scalar1=-1.0)
+            nc.vector.tensor_tensor(
+                out=x_t[:],
+                in0=fe[:, :, 0:DT2].unsqueeze(2).to_broadcast([P, 2, 8, DT2]),
+                in1=ident_b[:, 0:8].unsqueeze(1).unsqueeze(3).to_broadcast([P, 2, 8, DT2]),
+                op=ALU.mult,
+            )
+            nc.vector.tensor_copy(
+                out=selr.rearrange("p a (b c) -> p (a b) c", c=16),
+                in_=ident_b[:, 0:16].unsqueeze(2).to_broadcast([P, 16, 16]),
+            )
+            nc.vector.tensor_copy(
+                out=selc.rearrange("p (a c) -> p a c", c=16), in_=ident_b[:, 0:16].unsqueeze(1).to_broadcast([P, 8, 16])
+            )
+
+        def setup_positions():
+            for cs, tag in ((0, "B0"), (1, "B1")):
+                ps_t = psum.tile([P, 512], F32, tag=tag, name="ps_t")
+                nc.tensor.matmul(
+                    out=ps_t[:, 0:352], lhsT=ones_b[:], rhs=x_t[:, cs].rearrange("p f d -> p (f d)"), start=True, stop=True
+                )
+                nc.scalar.copy(out=pos_t[:, cs].rearrange("p f d -> p (f d)"), in_=ps_t[:, 0:352])
+            ps_e = psum.tile([P, 512], F32, tag="acc", name="ps_e", bufs=2)
+            for par in range(2):
+                for cs in range(2):
+                    o0 = DRC * (2 * par + cs)
+                    nc.tensor.matmul(
+                        out=ps_e[:, o0 : o0 + 42], lhsT=selr[:, par, :], rhs=fe[:, cs, 44:86], start=True, stop=True
+                    )
+                    nc.tensor.matmul(
+                        out=ps_e[:, o0 + 42 : o0 + 84], lhsT=selc[:], rhs=fe[:, cs, 86:128], start=True, stop=True
+                    )
+            nc.tensor.matmul(out=ps_e[:, 336:344], lhsT=fsrc[:, 128:256], rhs=ident_b[:, 0:8], start=True, stop=True)
+            nc.scalar.copy(out=pos_rc.rearrange("p a c n -> p (a c n)"), in_=ps_e[:, 0:336])
+            nc.scalar.copy(out=b_col[:], in_=ps_e[:, 336:344])
 
         def build_tab_t(f):
             nc.gpsimd.tensor_tensor(
@@ -181,25 +197,19 @@ def tile_causalwanselfattention_pa_kernel(tc, x, W, b, g, freqs_cos, freqs_sin, 
             )
 
         def build_tab_rc(par):
-            nc.gpsimd.tensor_tensor(
+            eng = nc.vector if RC_ON_V else nc.gpsimd
+            eng.tensor_tensor(
                 out=tab_rc[:, par],
                 in0=g_b3[:, :, DT2:P].unsqueeze(1).to_broadcast([P, 2, NH, DRC]),
                 in1=pos_rc[:, par].unsqueeze(2).to_broadcast([P, 2, NH, DRC]),
                 op=ALU.mult,
             )
 
-        build_tab_t(0)
-        build_tab_rc(0)
-        build_tab_rc(1)
-        for f in range(1, 8):
-            build_tab_t(f)
-
         ysb_tiles = {}
+        acc_of = {}
 
-        def mx_head(c, h):
-            if h == 0:
-                ysb_tiles[c] = ypool.tile([P, NH, 512], F32, tag="ysb", name="ysb")
-            acc = psum.tile([P, 512], F32, tag="acc", name="acc")
+        def mx(c, h):
+            acc = psum.tile([P, 512], F32, tag="acc", name="acc", bufs=2)
             for gi in range(2):
                 nc.tensor.matmul_mx(
                     out=acc[:],
@@ -210,73 +220,155 @@ def tile_causalwanselfattention_pa_kernel(tc, x, W, b, g, freqs_cos, freqs_sin, 
                     start=(gi == 0),
                     stop=(gi == 1),
                 )
+            acc_of[(c, h)] = acc
+
+        def sa(c, h):
+            if h == 0:
+                ysb_tiles[c] = ypool.tile([P, NH, 512], F32, tag="ysb", name="ysb")
             nc.scalar.activation(
-                out=ysb_tiles[c][:, h, :], in_=acc[:], func=ACT.Identity, bias=b_col[:, h : h + 1], scale=1.0
+                out=ysb_tiles[c][:, h, :], in_=acc_of[(c, h)][:], func=ACT.Identity, bias=b_col[:, h : h + 1], scale=1.0
             )
 
-        for h in range(NH):
-            w_tile_in(h, h % 2 == 0)
-            w_quant(h)
-            mx_head(0, h)
-        for t in range(4, 8):
-            x_tile_in(t, t % 2 == 0)
-        x_quant(1)
+        def mxsa(c, heads):
+            for h in heads:
+                mx(c, h)
+                sa(c, h)
 
-        def back_transposes(c, tt):
+        banks_of = {}
+        rstd_of = {}
+        prod_of = {}
+        SLOTS = ("A", "B", "A", "B", "A", "B", "A", "B", "C", "A", "B", "C", "A", "B", "C", "A")
+
+        def bt(i):
+            c, tt = divmod(i, 4)
             banks = []
             for bk in range(2):
-                yt = psum.tile([P, 512], F32, tag="yT%d" % bk, name="yT%d" % bk)
+                yt = psum.tile([P, 512], F32, tag="%s%d" % (SLOTS[i], bk), name="yT%d" % bk)
                 for hh in range(4):
                     nc.tensor.transpose(
                         yt[:, P * hh : P * (hh + 1)], ysb_tiles[c][:, 4 * bk + hh, P * tt : P * (tt + 1)], ident_f[:]
                     )
                 banks.append(yt)
-            return banks
+            banks_of[i] = banks
 
-        def epilogue(c, tt, banks):
-            t = 4 * c + tt
-            f, par = divmod(t, 2)
+        def sq(i):
             ss = small.tile([P, 4], F32, tag="ss", name="ss")
             for bk in range(2):
                 junk = work.tile([P, 512], F32, tag="junk", name="junk", bufs=2)
                 nc.scalar.activation(
-                    out=junk[:], in_=banks[bk][:], func=ACT.Square, scale=0.03125, accum_out=ss[:, bk : bk + 1]
+                    out=junk[:], in_=banks_of[i][bk][:], func=ACT.Square, scale=0.03125, accum_out=ss[:, bk : bk + 1]
                 )
             nc.scalar.activation(out=ss[:, 2:3], in_=ss[:, 1:2], func=ACT.Identity, bias=EPS, scale=1.0)
-            nc.scalar.activation(out=ss[:, 3:4], in_=ss[:, 0:1], func=ACT.Sqrt, bias=ss[:, 2:3], scale=1.0)
-            rstd = small.tile([P, 1], F32, tag="rstd", name="rstd")
-            nc.vector.reciprocal(out=rstd[:], in_=ss[:, 3:4])
+            nc.scalar.activation(
+                out=ss[:, 3:4], in_=ss[:, 0:1], func=ACT.Abs_reciprocal_sqrt, bias=ss[:, 2:3], scale=1.0
+            )
+            rstd_of[i] = ss[:, 3:4]
+
+        def stt(i):
+            f, par = divmod(i, 2)
             t1 = work.tile([P, NH, P], F32, tag="t1", name="t1")
             t2 = work.tile([P, NH, P], F32, tag="t2", name="t2")
             for bk in range(2):
-                y3 = banks[bk].rearrange("p (h d) -> p h d", d=P)
+                y3 = banks_of[i][bk].rearrange("p (h d) -> p h d", d=P)
                 hs = slice(4 * bk, 4 * bk + 4)
                 for cs, dst in ((0, t1), (1, t2)):
-                    nc.vector.scalar_tensor_tensor(
-                        out=dst[:, hs, 0:DT2], in0=y3[:, :, 0:DT2], scalar=rstd[:, 0:1],
-                        in1=tab_t[:, f, cs, hs, :], op0=ALU.mult, op1=ALU.mult,
-                    )
-                    nc.vector.scalar_tensor_tensor(
-                        out=dst[:, hs, DT2:P], in0=y3[:, :, DT2:P], scalar=rstd[:, 0:1],
-                        in1=tab_rc[:, par, cs, hs, :], op0=ALU.mult, op1=ALU.mult,
-                    )
-            o = work.tile([P, K], F32, tag="o", name="o")
+                    for lo, hi, tab in ((0, DT2, tab_t[:, f, cs, hs, :]), (DT2, P, tab_rc[:, par, cs, hs, :])):
+                        nc.vector.scalar_tensor_tensor(
+                            out=dst[:, hs, lo:hi], in0=tab, scalar=rstd_of[i], in1=y3[:, :, lo:hi],
+                            op0=ALU.mult, op1=ALU.mult,
+                        )
+            prod_of[i] = (t1, t2)
+
+        def add_half(i, o, half, eng):
+            t1, t2 = prod_of[i]
+            hs = slice(4 * half, 4 * half + 4)
+            cols = slice(512 * half, 512 * (half + 1))
+            eng.tensor_tensor(
+                out=o[:, cols].rearrange("p (n e) -> p n e", e=2),
+                in0=t1[:, hs, :].rearrange("p h (j e) -> p (h j) e", e=2),
+                in1=t2[:, hs, :].rearrange("p h (j e) -> p (h j) e", e=2)[:, :, ::-1],
+                op=ALU.add,
+            )
+            nc.sync.dma_start(out=out_rows[P * i : P * (i + 1), cols], in_=o[:, cols])
+
+        def add_store(i):
+            t1, t2 = prod_of[i]
+            o = work.tile([P, K], F32, tag="o", name="o", bufs=3)
+            if i == 15:
+                add_half(i, o, 0, nc.gpsimd)
+                add_half(i, o, 1, nc.vector)
+                return
             nc.gpsimd.tensor_tensor(
                 out=o.rearrange("p (n e) -> p n e", e=2),
                 in0=t1.rearrange("p h (j e) -> p (h j) e", e=2),
                 in1=t2.rearrange("p h (j e) -> p (h j) e", e=2)[:, :, ::-1],
                 op=ALU.add,
             )
-            nc.sync.dma_start(out=out_rows[P * t : P * (t + 1), :], in_=o[:])
+            nc.sync.dma_start(out=out_rows[P * i : P * (i + 1), :], in_=o[:])
 
-        for c in range(NCH):
-            for tt in range(4):
-                banks = back_transposes(c, tt)
-                if c + 1 < NCH:
-                    mx_head(c + 1, 2 * tt)
-                    mx_head(c + 1, 2 * tt + 1)
-                if c + 2 < NCH:
-                    x_tile_in(4 * (c + 2) + tt, tt % 2 == 0)
-                    if tt == 3:
-                        x_quant(c + 2)
-                epilogue(c, tt, banks)
+        setup_gain_bias()
+        setup_vector()
+        tc_in("x0", "C0")
+        tc_in("x1", "C1")
+        setup_positions()
+        build_tab_t(0)
+        if not RC_ON_V:
+            build_tab_rc(0)
+            build_tab_rc(1)
+        for f in range(1, TABS_HEAD):
+            build_tab_t(f)
+        tc_in("x2", "C0")
+        tc_in("x3", "C1")
+        tc_in("w0", "B0")
+        tc_in("w1", "B1")
+        q_x(0)
+        tc_in("w2", "C0")
+        q_w(0)
+        tc_in("w3", "C1")
+        q_w(1)
+        mxsa(0, (0, 1))
+        tc_in("w4", "B0")
+        q_w(2)
+        tc_in("w5", "B1")
+        q_w(3)
+        mxsa(0, (2, 3))
+        tc_in("w6", "C0")
+        q_w(4)
+        tc_in("w7", "C1")
+        q_w(5)
+        mxsa(0, (4, 5))
+        q_w(6)
+        q_w(7)
+        tc_in("x4", "B0")
+        tc_in("x5", "B1")
+        mxsa(0, (6, 7))
+        if RC_ON_V:
+            build_tab_rc(0)
+            build_tab_rc(1)
+        tc_in("x6", "C0")
+        tc_in("x7", "C1")
+
+        EXTRA_MX = {1: (0, 1, 2), 2: (3, 4, 5), 3: (6, 7)}
+        EXTRA_T = {0: (8,), 1: (9,), 2: (10,), 3: (11,), 4: (12,), 5: (13,), 6: (14,), 7: (15,)}
+        next_tab = TABS_HEAD
+        for i in range(16):
+            c, tt = divmod(i, 4)
+            bt(i)
+            sq(i)
+            if i == 0:
+                q_x(1)
+            if c == 0:
+                mxsa(1, EXTRA_MX.get(i, ()))
+            elif c + 1 < NCH:
+                mxsa(c + 1, (2 * tt, 2 * tt + 1))
+            for t in EXTRA_T.get(i, ()):
+                tc_in("x%d" % t, "C%d" % (t % 2))
+            stt(i)
+            if i == 3:
+                q_x(2)
+            if i == 7:
+                q_x(3)
+            add_store(i)
+            if next_tab < 8:
+                build_tab_t(next_tab)
+                next_tab += 1

@@ -20,10 +20,40 @@ NCH = 4
 EPS = 1e-6
 DT2 = 44
 DRC = 84
-MANUAL = False
-RC_ON_V = True
-TABS_HEAD = 8
-V_COPIES = ()
+SLOTS = ("A", "B", "A", "B", "A", "B", "A", "B", "C", "A", "B", "C", "A", "B", "C", "A")
+ORDER = (
+    "gain 0", "vec", "gain 1", "gainS 0", "t x0 C0", "gainS 1", "t x1 C1", "c x0 V", "posT 1", "c x1 S", "posT 0",
+    "posRC 0", "posTS 1", "posTS 0", "t x2 C0", "posRCS 0", "tabT 0 G", "t x3 C1", "c x2 V", "t w0 B0", "c x3 S",
+    "t w1 B1", "c w0 V", "tabT 1 G", "t w2 C0", "c w1 S", "t w3 C1", "c w2 V", "t w4 B0", "c w3 S", "t w5 B1",
+    "qx 0 0", "t w6 C0", "qx 0 1", "t w7 C1", "qw 0", "qw 1", "mx 0 0 1", "qw 2", "c w5 S", "qw 3", "mx 0 1 0",
+    "c w4 V", "tabT 2 G", "sa 0 0", "t x5 B1", "c w6 V", "sa 0 1", "t x4 B0", "c w7 S", "t x6 C0", "qw 4",
+    "c x4 S", "qw 5", "t x7 C1", "c x6 S", "qw 6", "qw 7", "mx 0 2 1", "c x5 S", "tabRC 0 V", "mx 0 3 0", "c x7 S",
+    "sa 0 2", "t x8 C0", "tabRC 1 V", "sa 0 3", "t x9 C1", "c x8 S", "mx 0 4 1", "mx 0 5 0", "qx 1 0", "sa 0 4",
+    "qx 1 1", "bt 0 0", "sa 0 5", "bt 1 0", "tabT 3 G", "c x9 V", "sq 0 0", "t x10 C0", "sq 1 0", "t x11 C1",
+    "c x10 S", "mx 0 6 1", "tabT 4 G", "c x11 S", "mx 0 7 0", "sa 0 6", "t x12 C0", "sa 0 7", "t x13 C1", "qx 2 1",
+    "c x12 S", "bt 0 1", "bt 1 1", "qx 2 0", "sq 0 1", "t x14 C0", "tabT 5 G", "c x13 V", "sq 1 1", "mx 1 1 0",
+    "tiny1 0", "c x14 S", "mx 1 0 1", "tiny2 0", "tiny1 1", "sa 1 1", "stt 0 0", "t x15 C1", "tabT 6 G", "tiny2 1",
+    "sa 1 0", "mx 1 3 0", "stt 0 1", "c x15 S", "mx 1 2 1", "sa 1 3", "tabT 7 G", "bt 2 0", "stt 1 1", "sa 1 2",
+    "bt 2 1", "mx 1 5 0", "sq 2 1", "mx 1 4 1", "stt 1 0", "sq 2 0", "add 0", "tiny1 2", "bt 3 1", "sa 1 5",
+    "tiny2 2", "bt 3 0", "sq 3 1", "stt 2 0", "mx 1 7 0", "sa 1 4", "tiny1 3", "add 1", "sq 3 0", "stt 2 1",
+    "mx 1 6 1", "st 0", "sa 1 7", "bt 4 0", "tiny2 3", "sa 1 6", "mx 2 1 0", "stt 3 0", "sq 4 0", "bt 4 1",
+    "add 2", "mx 2 0 1", "st 1", "sq 4 1", "stt 3 1", "sa 2 1", "bt 5 0", "tiny1 4", "sq 5 0", "mx 2 3 0",
+    "tiny2 4", "sa 2 0", "bt 5 1", "stt 4 0", "add 3", "st 2", "sq 5 1", "mx 2 2 1", "sa 2 3", "stt 4 1", "bt 6 0",
+    "tiny1 5", "sa 2 2", "mx 2 5 0", "tiny2 5", "sq 6 0", "mx 2 4 1", "stt 5 0", "add 4", "st 3", "sa 2 5",
+    "bt 6 1", "bt 8 0", "sq 6 1", "stt 5 1", "bt 7 0", "sa 2 4", "mx 2 7 0", "tiny1 6", "sq 7 0", "mx 2 6 1",
+    "qx 3 0", "st 4", "tiny2 6", "sa 2 7", "bt 7 1", "add 5", "stt 6 0", "sq 7 1", "sa 2 6", "stt 6 1", "bt 9 0",
+    "tiny1 7", "sq 8 0", "bt 8 1", "tiny2 7", "qx 3 1", "sq 8 1", "st 5", "bt 9 1", "add 6", "stt 7 0", "sq 9 1",
+    "mx 3 0 1", "tiny1 8", "mx 3 1 0", "sq 9 0", "stt 7 1", "tiny2 8", "bt 10 0", "tiny1 9", "sa 3 1", "tiny2 9",
+    "sa 3 0", "mx 3 3 0", "stt 8 0", "add 7", "st 6", "sq 10 0", "bt 10 1", "mx 3 2 1", "sq 10 1", "stt 8 1",
+    "sa 3 3", "bt 11 0", "tiny1 10", "sa 3 2", "mx 3 5 0", "stt 9 0", "add 8", "st 7", "tiny2 10", "sq 11 0",
+    "mx 3 4 1", "stt 9 1", "sa 3 5", "bt 11 1", "bt 12 0", "sa 3 4", "mx 3 7 0", "stt 10 0", "sq 11 1", "add 9",
+    "mx 3 6 1", "st 8", "sa 3 7", "stt 10 1", "tiny1 11", "sa 3 6", "bt 13 0", "tiny2 11", "sq 12 0", "bt 12 1",
+    "stt 11 0", "bt 13 1", "sq 12 1", "add 10", "st 9", "sq 13 1", "stt 11 1", "bt 14 0", "tiny1 12", "sq 13 0",
+    "tiny2 12", "tiny1 13", "sq 14 0", "stt 12 0", "bt 14 1", "add 11", "st 10", "tiny2 13", "sq 14 1", "stt 12 1",
+    "bt 15 0", "tiny1 14", "tiny2 14", "sq 15 0", "stt 13 0", "bt 15 1", "add 12", "st 11", "sq 15 1", "stt 13 1",
+    "tiny1 15", "tiny2 15", "stt 14 0", "add 13", "st 12", "stt 14 1", "stt 15 0", "add 14", "st 13", "stt 15 1",
+    "addh 15 0 G", "st 14", "addh 15 1 V", "sth 15 0", "sth 15 1",
+)
 
 
 def tile_causalwanselfattention_pa_kernel(tc, x, W, b, g, freqs_cos, freqs_sin, out):
@@ -39,8 +69,16 @@ def tile_causalwanselfattention_pa_kernel(tc, x, W, b, g, freqs_cos, freqs_sin, 
         work = ctx.enter_context(tc.tile_pool(name="work", bufs=4))
         small = ctx.enter_context(tc.tile_pool(name="small", bufs=4))
         psum = ctx.enter_context(tc.psum_pool(name="psum", bufs=1))
-        if MANUAL:
-            ctx.enter_context(tc.manual_schedule())
+        ctx.enter_context(tc.manual_schedule())
+
+        def eng_of(name):
+            return {"V": nc.vector, "G": nc.gpsimd, "S": nc.scalar}[name]
+
+        def copy_on(name, dst, srcv):
+            if name == "S":
+                nc.scalar.copy(out=dst, in_=srcv)
+            else:
+                nc.vector.tensor_copy(out=dst, in_=srcv)
 
         fsrc = const.tile([P, 384], BF16, name="fsrc")
         nc.vector.memset(fsrc[:], 0.0)
@@ -77,53 +115,6 @@ def tile_causalwanselfattention_pa_kernel(tc, x, W, b, g, freqs_cos, freqs_sin, 
         ws = const.tile([P, NH, 2, P], U8, name="ws", align_bytes=64)
         xc = const.tile([P, NCH, 2, 512], U32, name="xc", align_bytes=64)
         xs = const.tile([P, NCH, 2, 512], U8, name="xs", align_bytes=64)
-
-        xt_of = {}
-        xg_tiles = {}
-        wg_tiles = {}
-
-        def t_in(key, tag):
-            words = raw_tiles[key].bitcast(F32)
-            xt = psum.tile([P, 2, 2, P], F32, tag=tag, name="xt_" + key)
-            for gi in range(2):
-                for u in range(2):
-                    nc.tensor.transpose(xt[:, gi, u, :], words[:, 256 * gi + u : 256 * (gi + 1) : 2], ident_f[:])
-            xt_of[key] = xt
-
-        def c_in(key):
-            n = int(key[1:])
-            if key[0] == "x":
-                c, tt = divmod(n, 4)
-                if tt == 0:
-                    xg_tiles[c] = grp.tile([P, 2, 2048], BF16, tag="xg", name="xg", align_bytes=64)
-                dst = xg_tiles[c].bitcast(F32)[:, :, 256 * tt : 256 * (tt + 1)]
-            else:
-                wg_tiles[n] = grp.tile([P, 2, 512], BF16, tag="wg", name="wg", align_bytes=64, bufs=4)
-                dst = wg_tiles[n].bitcast(F32)
-            dst = dst.rearrange("p g (r u) -> p g r u", u=2)
-            srcv = xt_of[key].rearrange("p g u r -> p g r u")
-            if key in V_COPIES:
-                nc.vector.tensor_copy(out=dst, in_=srcv)
-            else:
-                nc.scalar.copy(out=dst, in_=srcv)
-
-        def tc_in(key, tag):
-            t_in(key, tag)
-            c_in(key)
-
-        def q_x(c):
-            for gi in range(2):
-                nc.vector.quantize_mx(
-                    out=xc[:, c, gi, :].bitcast(FP8X4), scales=xs[:, c, gi, :], in_=xg_tiles[c][:, gi, :]
-                )
-
-        def q_w(h):
-            nc.vector.quantize_mx(
-                out=wc[:, h].rearrange("p g m -> p (g m)").bitcast(FP8X4),
-                scales=ws[:, h].rearrange("p g m -> p (g m)"),
-                in_=wg_tiles[h].rearrange("p g n -> p (g n)"),
-            )
-
         g_b = const.tile([P, K], F32, name="g_b")
         pos_t = const.tile([P, 2, 8, DT2], F32, name="pos_t")
         pos_rc = const.tile([P, 2, 2, DRC], F32, name="pos_rc")
@@ -136,45 +127,57 @@ def tile_causalwanselfattention_pa_kernel(tc, x, W, b, g, freqs_cos, freqs_sin, 
         tab_t = const.tile([P, 8, 2, NH, DT2], F32, name="tab_t")
         tab_rc = const.tile([P, 2, 2, NH, DRC], F32, name="tab_rc")
 
-        def setup_gain_bias():
-            for half, tag in ((0, "A0"), (1, "A1")):
-                ps_g = psum.tile([P, 512], F32, tag=tag, name="ps_g")
-                for hh in range(4):
-                    h = 4 * half + hh
-                    nc.tensor.matmul(
-                        out=ps_g[:, P * hh : P * (hh + 1)], lhsT=ident_b[:, h : h + 1].to_broadcast([P, P]),
-                        rhs=fsrc[:, 256:384], start=True, stop=True,
-                    )
-                nc.scalar.copy(out=g_b[:, 512 * half : 512 * (half + 1)], in_=ps_g[:])
+        live = {}
 
-        def setup_vector():
+        def op_gain(half):
+            half = int(half)
+            ps_g = psum.tile([P, 512], F32, tag="A%d" % half, name="ps_g")
+            for hh in range(4):
+                h = 4 * half + hh
+                nc.tensor.matmul(
+                    out=ps_g[:, P * hh : P * (hh + 1)], lhsT=ident_b[:, h : h + 1].to_broadcast([P, P]),
+                    rhs=fsrc[:, 256:384], start=True, stop=True,
+                )
+            live[("g", half)] = ps_g
+
+        def op_gainS(half, eng="S"):
+            half = int(half)
+            copy_on(eng, g_b[:, 512 * half : 512 * (half + 1)], live[("g", half)][:])
+
+        def op_vec():
             nc.vector.tensor_copy(
                 out=fe.rearrange("p c (j e) -> p (c j) e", e=2), in_=fsrc[:, 0:128].unsqueeze(2).to_broadcast([P, P, 2])
             )
+            nc.vector.tensor_copy(
+                out=selr.rearrange("p a (b c) -> p (a b) c", c=16),
+                in_=ident_b[:, 0:16].unsqueeze(2).to_broadcast([P, 16, 16]),
+            )
             sin_odd = fe.rearrange("p c (j e) -> p c j e", e=2)[:, 1, :, 1:2]
             nc.vector.tensor_scalar_mul(out=sin_odd, in0=sin_odd, scalar1=-1.0)
+            nc.vector.tensor_copy(
+                out=selc.rearrange("p (a c) -> p a c", c=16), in_=ident_b[:, 0:16].unsqueeze(1).to_broadcast([P, 8, 16])
+            )
             nc.vector.tensor_tensor(
                 out=x_t[:],
                 in0=fe[:, :, 0:DT2].unsqueeze(2).to_broadcast([P, 2, 8, DT2]),
                 in1=ident_b[:, 0:8].unsqueeze(1).unsqueeze(3).to_broadcast([P, 2, 8, DT2]),
                 op=ALU.mult,
             )
-            nc.vector.tensor_copy(
-                out=selr.rearrange("p a (b c) -> p (a b) c", c=16),
-                in_=ident_b[:, 0:16].unsqueeze(2).to_broadcast([P, 16, 16]),
-            )
-            nc.vector.tensor_copy(
-                out=selc.rearrange("p (a c) -> p a c", c=16), in_=ident_b[:, 0:16].unsqueeze(1).to_broadcast([P, 8, 16])
-            )
 
-        def setup_positions():
-            for cs, tag in ((0, "B0"), (1, "B1")):
-                ps_t = psum.tile([P, 512], F32, tag=tag, name="ps_t")
-                nc.tensor.matmul(
-                    out=ps_t[:, 0:352], lhsT=ones_b[:], rhs=x_t[:, cs].rearrange("p f d -> p (f d)"), start=True, stop=True
-                )
-                nc.scalar.copy(out=pos_t[:, cs].rearrange("p f d -> p (f d)"), in_=ps_t[:, 0:352])
-            ps_e = psum.tile([P, 512], F32, tag="acc", name="ps_e", bufs=2)
+        def op_posT(cs):
+            cs = int(cs)
+            ps_t = psum.tile([P, 512], F32, tag="B%d" % cs, name="ps_t")
+            nc.tensor.matmul(
+                out=ps_t[:, 0:352], lhsT=ones_b[:], rhs=x_t[:, cs].rearrange("p f d -> p (f d)"), start=True, stop=True
+            )
+            live[("pt", cs)] = ps_t
+
+        def op_posTS(cs, eng="S"):
+            cs = int(cs)
+            copy_on(eng, pos_t[:, cs].rearrange("p f d -> p (f d)"), live[("pt", cs)][:, 0:352])
+
+        def op_posRC(k):
+            ps_e = psum.tile([P, 512], F32, tag="acc" + k, name="ps_e")
             for par in range(2):
                 for cs in range(2):
                     o0 = DRC * (2 * par + cs)
@@ -185,31 +188,67 @@ def tile_causalwanselfattention_pa_kernel(tc, x, W, b, g, freqs_cos, freqs_sin, 
                         out=ps_e[:, o0 + 42 : o0 + 84], lhsT=selc[:], rhs=fe[:, cs, 86:128], start=True, stop=True
                     )
             nc.tensor.matmul(out=ps_e[:, 336:344], lhsT=fsrc[:, 128:256], rhs=ident_b[:, 0:8], start=True, stop=True)
-            nc.scalar.copy(out=pos_rc.rearrange("p a c n -> p (a c n)"), in_=ps_e[:, 0:336])
-            nc.scalar.copy(out=b_col[:], in_=ps_e[:, 336:344])
+            live["pe"] = ps_e
 
-        def build_tab_t(f):
-            nc.gpsimd.tensor_tensor(
+        def op_posRCS(k, eng="S"):
+            copy_on(eng, b_col[:], live["pe"][:, 336:344])
+            copy_on(eng, pos_rc.rearrange("p a c n -> p (a c n)"), live["pe"][:, 0:336])
+
+        def op_tabT(f, eng="G"):
+            f = int(f)
+            eng_of(eng).tensor_tensor(
                 out=tab_t[:, f],
                 in0=g_b3[:, :, 0:DT2].unsqueeze(1).to_broadcast([P, 2, NH, DT2]),
                 in1=pos_t[:, :, f, :].unsqueeze(2).to_broadcast([P, 2, NH, DT2]),
                 op=ALU.mult,
             )
 
-        def build_tab_rc(par):
-            eng = nc.vector if RC_ON_V else nc.gpsimd
-            eng.tensor_tensor(
+        def op_tabRC(par, eng="V"):
+            par = int(par)
+            eng_of(eng).tensor_tensor(
                 out=tab_rc[:, par],
                 in0=g_b3[:, :, DT2:P].unsqueeze(1).to_broadcast([P, 2, NH, DRC]),
                 in1=pos_rc[:, par].unsqueeze(2).to_broadcast([P, 2, NH, DRC]),
                 op=ALU.mult,
             )
 
-        ysb_tiles = {}
-        acc_of = {}
+        def op_t(key, tag):
+            words = raw_tiles[key].bitcast(F32)
+            xt = psum.tile([P, 2, 2, P], F32, tag=tag, name="xt_" + key)
+            for gi in range(2):
+                for u in range(2):
+                    nc.tensor.transpose(xt[:, gi, u, :], words[:, 256 * gi + u : 256 * (gi + 1) : 2], ident_f[:])
+            live[("xt", key)] = xt
 
-        def mx(c, h):
-            acc = psum.tile([P, 512], F32, tag="acc", name="acc", bufs=2)
+        def op_c(key, eng):
+            n = int(key[1:])
+            if key[0] == "x":
+                c, tt = divmod(n, 4)
+                if ("xg", c) not in live:
+                    live[("xg", c)] = grp.tile([P, 2, 2048], BF16, tag="xg", name="xg", align_bytes=64)
+                dst = live[("xg", c)].bitcast(F32)[:, :, 256 * tt : 256 * (tt + 1)]
+            else:
+                live[("wg", n)] = grp.tile([P, 2, 512], BF16, tag="wg", name="wg", align_bytes=64, bufs=4)
+                dst = live[("wg", n)].bitcast(F32)
+            copy_on(eng, dst.rearrange("p g (r u) -> p g r u", u=2), live[("xt", key)].rearrange("p g u r -> p g r u"))
+
+        def op_qx(c, gi):
+            c, gi = int(c), int(gi)
+            nc.vector.quantize_mx(
+                out=xc[:, c, gi, :].bitcast(FP8X4), scales=xs[:, c, gi, :], in_=live[("xg", c)][:, gi, :]
+            )
+
+        def op_qw(h):
+            h = int(h)
+            nc.vector.quantize_mx(
+                out=wc[:, h].rearrange("p g m -> p (g m)").bitcast(FP8X4),
+                scales=ws[:, h].rearrange("p g m -> p (g m)"),
+                in_=live[("wg", h)].rearrange("p g n -> p (g n)"),
+            )
+
+        def op_mx(c, h, k):
+            c, h = int(c), int(h)
+            acc = psum.tile([P, 512], F32, tag="acc" + k, name="acc")
             for gi in range(2):
                 nc.tensor.matmul_mx(
                     out=acc[:],
@@ -220,155 +259,97 @@ def tile_causalwanselfattention_pa_kernel(tc, x, W, b, g, freqs_cos, freqs_sin, 
                     start=(gi == 0),
                     stop=(gi == 1),
                 )
-            acc_of[(c, h)] = acc
+            live[("acc", c, h)] = acc
 
-        def sa(c, h):
-            if h == 0:
-                ysb_tiles[c] = ypool.tile([P, NH, 512], F32, tag="ysb", name="ysb")
+        def op_sa(c, h):
+            c, h = int(c), int(h)
+            if ("ysb", c) not in live:
+                live[("ysb", c)] = ypool.tile([P, NH, 512], F32, tag="ysb", name="ysb")
             nc.scalar.activation(
-                out=ysb_tiles[c][:, h, :], in_=acc_of[(c, h)][:], func=ACT.Identity, bias=b_col[:, h : h + 1], scale=1.0
+                out=live[("ysb", c)][:, h, :], in_=live[("acc", c, h)][:], func=ACT.Identity,
+                bias=b_col[:, h : h + 1], scale=1.0,
             )
 
-        def mxsa(c, heads):
-            for h in heads:
-                mx(c, h)
-                sa(c, h)
-
-        banks_of = {}
-        rstd_of = {}
-        prod_of = {}
-        SLOTS = ("A", "B", "A", "B", "A", "B", "A", "B", "C", "A", "B", "C", "A", "B", "C", "A")
-
-        def bt(i):
+        def op_bt(i, bk):
+            i, bk = int(i), int(bk)
             c, tt = divmod(i, 4)
-            banks = []
-            for bk in range(2):
-                yt = psum.tile([P, 512], F32, tag="%s%d" % (SLOTS[i], bk), name="yT%d" % bk)
-                for hh in range(4):
-                    nc.tensor.transpose(
-                        yt[:, P * hh : P * (hh + 1)], ysb_tiles[c][:, 4 * bk + hh, P * tt : P * (tt + 1)], ident_f[:]
-                    )
-                banks.append(yt)
-            banks_of[i] = banks
-
-        def sq(i):
-            ss = small.tile([P, 4], F32, tag="ss", name="ss")
-            for bk in range(2):
-                junk = work.tile([P, 512], F32, tag="junk", name="junk", bufs=2)
-                nc.scalar.activation(
-                    out=junk[:], in_=banks_of[i][bk][:], func=ACT.Square, scale=0.03125, accum_out=ss[:, bk : bk + 1]
+            yt = psum.tile([P, 512], F32, tag="%s%d" % (SLOTS[i], bk), name="yT%d" % bk)
+            for hh in range(4):
+                nc.tensor.transpose(
+                    yt[:, P * hh : P * (hh + 1)], live[("ysb", c)][:, 4 * bk + hh, P * tt : P * (tt + 1)], ident_f[:]
                 )
+            live[("yt", i, bk)] = yt
+
+        def op_sq(i, bk):
+            i, bk = int(i), int(bk)
+            if ("ss", i) not in live:
+                live[("ss", i)] = small.tile([P, 4], F32, tag="ss", name="ss")
+            junk = work.tile([P, 512], F32, tag="junk", name="junk", bufs=2)
+            nc.scalar.activation(
+                out=junk[:], in_=live[("yt", i, bk)][:], func=ACT.Square, scale=0.03125,
+                accum_out=live[("ss", i)][:, bk : bk + 1],
+            )
+
+        def op_tiny1(i):
+            ss = live[("ss", int(i))]
             nc.scalar.activation(out=ss[:, 2:3], in_=ss[:, 1:2], func=ACT.Identity, bias=EPS, scale=1.0)
+
+        def op_tiny2(i):
+            ss = live[("ss", int(i))]
             nc.scalar.activation(
                 out=ss[:, 3:4], in_=ss[:, 0:1], func=ACT.Abs_reciprocal_sqrt, bias=ss[:, 2:3], scale=1.0
             )
-            rstd_of[i] = ss[:, 3:4]
 
-        def stt(i):
+        def op_stt(i, bk):
+            i, bk = int(i), int(bk)
             f, par = divmod(i, 2)
-            t1 = work.tile([P, NH, P], F32, tag="t1", name="t1")
-            t2 = work.tile([P, NH, P], F32, tag="t2", name="t2")
-            for bk in range(2):
-                y3 = banks_of[i][bk].rearrange("p (h d) -> p h d", d=P)
-                hs = slice(4 * bk, 4 * bk + 4)
-                for cs, dst in ((0, t1), (1, t2)):
-                    for lo, hi, tab in ((0, DT2, tab_t[:, f, cs, hs, :]), (DT2, P, tab_rc[:, par, cs, hs, :])):
-                        nc.vector.scalar_tensor_tensor(
-                            out=dst[:, hs, lo:hi], in0=tab, scalar=rstd_of[i], in1=y3[:, :, lo:hi],
-                            op0=ALU.mult, op1=ALU.mult,
-                        )
-            prod_of[i] = (t1, t2)
+            if ("t", i) not in live:
+                t1 = work.tile([P, NH, P], F32, tag="t1", name="t1")
+                t2 = work.tile([P, NH, P], F32, tag="t2", name="t2")
+                live[("t", i)] = (t1, t2)
+            y3 = live[("yt", i, bk)].rearrange("p (h d) -> p h d", d=P)
+            hs = slice(4 * bk, 4 * bk + 4)
+            for cs in range(2):
+                dst = live[("t", i)][cs]
+                for lo, hi, tab in ((0, DT2, tab_t[:, f, cs, hs, :]), (DT2, P, tab_rc[:, par, cs, hs, :])):
+                    nc.vector.scalar_tensor_tensor(
+                        out=dst[:, hs, lo:hi], in0=tab, scalar=live[("ss", i)][:, 3:4], in1=y3[:, :, lo:hi],
+                        op0=ALU.mult, op1=ALU.mult,
+                    )
 
-        def add_half(i, o, half, eng):
-            t1, t2 = prod_of[i]
-            hs = slice(4 * half, 4 * half + 4)
-            cols = slice(512 * half, 512 * (half + 1))
-            eng.tensor_tensor(
-                out=o[:, cols].rearrange("p (n e) -> p n e", e=2),
+        def add_part(i, hs, cols, eng):
+            if ("o", i) not in live:
+                live[("o", i)] = work.tile([P, K], F32, tag="o", name="o", bufs=3)
+            t1, t2 = live[("t", i)]
+            eng_of(eng).tensor_tensor(
+                out=live[("o", i)][:, cols].rearrange("p (n e) -> p n e", e=2),
                 in0=t1[:, hs, :].rearrange("p h (j e) -> p (h j) e", e=2),
                 in1=t2[:, hs, :].rearrange("p h (j e) -> p (h j) e", e=2)[:, :, ::-1],
                 op=ALU.add,
             )
-            nc.sync.dma_start(out=out_rows[P * i : P * (i + 1), cols], in_=o[:, cols])
 
-        def add_store(i):
-            t1, t2 = prod_of[i]
-            o = work.tile([P, K], F32, tag="o", name="o", bufs=3)
-            if i == 15:
-                add_half(i, o, 0, nc.gpsimd)
-                add_half(i, o, 1, nc.vector)
-                return
-            nc.gpsimd.tensor_tensor(
-                out=o.rearrange("p (n e) -> p n e", e=2),
-                in0=t1.rearrange("p h (j e) -> p (h j) e", e=2),
-                in1=t2.rearrange("p h (j e) -> p (h j) e", e=2)[:, :, ::-1],
-                op=ALU.add,
-            )
-            nc.sync.dma_start(out=out_rows[P * i : P * (i + 1), :], in_=o[:])
+        def op_add(i):
+            add_part(int(i), slice(0, NH), slice(0, K), "G")
 
-        setup_gain_bias()
-        setup_vector()
-        tc_in("x0", "C0")
-        tc_in("x1", "C1")
-        setup_positions()
-        build_tab_t(0)
-        if not RC_ON_V:
-            build_tab_rc(0)
-            build_tab_rc(1)
-        for f in range(1, TABS_HEAD):
-            build_tab_t(f)
-        tc_in("x2", "C0")
-        tc_in("x3", "C1")
-        tc_in("w0", "B0")
-        tc_in("w1", "B1")
-        q_x(0)
-        tc_in("w2", "C0")
-        q_w(0)
-        tc_in("w3", "C1")
-        q_w(1)
-        mxsa(0, (0, 1))
-        tc_in("w4", "B0")
-        q_w(2)
-        tc_in("w5", "B1")
-        q_w(3)
-        mxsa(0, (2, 3))
-        tc_in("w6", "C0")
-        q_w(4)
-        tc_in("w7", "C1")
-        q_w(5)
-        mxsa(0, (4, 5))
-        q_w(6)
-        q_w(7)
-        tc_in("x4", "B0")
-        tc_in("x5", "B1")
-        mxsa(0, (6, 7))
-        if RC_ON_V:
-            build_tab_rc(0)
-            build_tab_rc(1)
-        tc_in("x6", "C0")
-        tc_in("x7", "C1")
+        def op_st(i):
+            i = int(i)
+            nc.sync.dma_start(out=out_rows[P * i : P * (i + 1), :], in_=live[("o", i)][:])
 
-        EXTRA_MX = {1: (0, 1, 2), 2: (3, 4, 5), 3: (6, 7)}
-        EXTRA_T = {0: (8,), 1: (9,), 2: (10,), 3: (11,), 4: (12,), 5: (13,), 6: (14,), 7: (15,)}
-        next_tab = TABS_HEAD
-        for i in range(16):
-            c, tt = divmod(i, 4)
-            bt(i)
-            sq(i)
-            if i == 0:
-                q_x(1)
-            if c == 0:
-                mxsa(1, EXTRA_MX.get(i, ()))
-            elif c + 1 < NCH:
-                mxsa(c + 1, (2 * tt, 2 * tt + 1))
-            for t in EXTRA_T.get(i, ()):
-                tc_in("x%d" % t, "C%d" % (t % 2))
-            stt(i)
-            if i == 3:
-                q_x(2)
-            if i == 7:
-                q_x(3)
-            add_store(i)
-            if next_tab < 8:
-                build_tab_t(next_tab)
-                next_tab += 1
+        def op_addh(i, bk, eng):
+            bk = int(bk)
+            add_part(int(i), slice(4 * bk, 4 * bk + 4), slice(512 * bk, 512 * (bk + 1)), eng)
+
+        def op_sth(i, bk):
+            i, bk = int(i), int(bk)
+            cols = slice(512 * bk, 512 * (bk + 1))
+            nc.sync.dma_start(out=out_rows[P * i : P * (i + 1), cols], in_=live[("o", i)][:, cols])
+
+        ops = {
+            "gain": op_gain, "gainS": op_gainS, "vec": op_vec, "posT": op_posT, "posTS": op_posTS, "posRC": op_posRC,
+            "posRCS": op_posRCS, "tabT": op_tabT, "tabRC": op_tabRC, "t": op_t, "c": op_c, "qx": op_qx, "qw": op_qw,
+            "mx": op_mx, "sa": op_sa, "bt": op_bt, "sq": op_sq, "tiny1": op_tiny1, "tiny2": op_tiny2, "stt": op_stt,
+            "add": op_add, "st": op_st, "addh": op_addh, "sth": op_sth,
+        }
+        for tok in ORDER:
+            parts = tok.split(" ")
+            ops[parts[0]](*parts[1:])

@@ -22,37 +22,38 @@ DT2 = 44
 DRC = 84
 SLOTS = ("A", "B", "A", "B", "A", "B", "A", "B", "C", "A", "B", "C", "A", "B", "C", "A")
 ORDER = (
-    "gain 0", "vec", "gain 1", "gainS 0", "t x0 C0", "gainS 1", "t x1 C1", "c x0 V", "posT 1", "c x1 S", "posT 0",
-    "posRC 0", "posTS 1", "posTS 0", "t x2 C0", "posRCS 0", "tabT 0 G", "t x3 C1", "c x2 V", "t w0 B0", "c x3 S",
-    "t w1 B1", "c w0 V", "tabT 1 G", "t w2 C0", "c w1 S", "t w3 C1", "c w2 V", "t w4 B0", "c w3 S", "t w5 B1",
-    "qx 0 0", "t w6 C0", "qx 0 1", "t w7 C1", "qw 0", "qw 1", "mx 0 0 1", "qw 2", "c w5 S", "qw 3", "mx 0 1 0",
-    "c w4 V", "tabT 2 G", "sa 0 0", "t x5 B1", "c w6 V", "sa 0 1", "t x4 B0", "c w7 S", "t x6 C0", "qw 4",
-    "c x4 S", "qw 5", "t x7 C1", "c x6 S", "qw 6", "qw 7", "mx 0 2 1", "c x5 S", "tabRC 0 V", "mx 0 3 0", "c x7 S",
-    "sa 0 2", "t x8 C0", "tabRC 1 V", "sa 0 3", "t x9 C1", "c x8 S", "mx 0 4 1", "mx 0 5 0", "qx 1 0", "sa 0 4",
-    "qx 1 1", "bt 0 0", "sa 0 5", "bt 1 0", "tabT 3 G", "c x9 V", "sq 0 0", "t x10 C0", "sq 1 0", "t x11 C1",
-    "c x10 S", "mx 0 6 1", "tabT 4 G", "c x11 S", "mx 0 7 0", "sa 0 6", "t x12 C0", "sa 0 7", "t x13 C1", "qx 2 1",
-    "c x12 S", "bt 0 1", "bt 1 1", "qx 2 0", "sq 0 1", "t x14 C0", "tabT 5 G", "c x13 V", "sq 1 1", "mx 1 1 0",
-    "tiny1 0", "c x14 S", "mx 1 0 1", "tiny2 0", "tiny1 1", "sa 1 1", "stt 0 0", "t x15 C1", "tabT 6 G", "tiny2 1",
-    "sa 1 0", "mx 1 3 0", "stt 0 1", "c x15 S", "mx 1 2 1", "sa 1 3", "tabT 7 G", "bt 2 0", "stt 1 1", "sa 1 2",
-    "bt 2 1", "mx 1 5 0", "sq 2 1", "mx 1 4 1", "stt 1 0", "sq 2 0", "add 0", "tiny1 2", "bt 3 1", "sa 1 5",
-    "tiny2 2", "bt 3 0", "sq 3 1", "stt 2 0", "mx 1 7 0", "sa 1 4", "tiny1 3", "add 1", "sq 3 0", "stt 2 1",
-    "mx 1 6 1", "st 0", "sa 1 7", "bt 4 0", "tiny2 3", "sa 1 6", "mx 2 1 0", "stt 3 0", "sq 4 0", "bt 4 1",
-    "add 2", "mx 2 0 1", "st 1", "sq 4 1", "stt 3 1", "sa 2 1", "bt 5 0", "tiny1 4", "sq 5 0", "mx 2 3 0",
-    "tiny2 4", "sa 2 0", "bt 5 1", "stt 4 0", "add 3", "st 2", "sq 5 1", "mx 2 2 1", "sa 2 3", "stt 4 1", "bt 6 0",
-    "tiny1 5", "sa 2 2", "mx 2 5 0", "tiny2 5", "sq 6 0", "mx 2 4 1", "stt 5 0", "add 4", "st 3", "sa 2 5",
-    "bt 6 1", "bt 8 0", "sq 6 1", "stt 5 1", "bt 7 0", "sa 2 4", "mx 2 7 0", "tiny1 6", "sq 7 0", "mx 2 6 1",
-    "qx 3 0", "st 4", "tiny2 6", "sa 2 7", "bt 7 1", "add 5", "stt 6 0", "sq 7 1", "sa 2 6", "stt 6 1", "bt 9 0",
-    "tiny1 7", "sq 8 0", "bt 8 1", "tiny2 7", "qx 3 1", "sq 8 1", "st 5", "bt 9 1", "add 6", "stt 7 0", "sq 9 1",
-    "mx 3 0 1", "tiny1 8", "mx 3 1 0", "sq 9 0", "stt 7 1", "tiny2 8", "bt 10 0", "tiny1 9", "sa 3 1", "tiny2 9",
-    "sa 3 0", "mx 3 3 0", "stt 8 0", "add 7", "st 6", "sq 10 0", "bt 10 1", "mx 3 2 1", "sq 10 1", "stt 8 1",
-    "sa 3 3", "bt 11 0", "tiny1 10", "sa 3 2", "mx 3 5 0", "stt 9 0", "add 8", "st 7", "tiny2 10", "sq 11 0",
-    "mx 3 4 1", "stt 9 1", "sa 3 5", "bt 11 1", "bt 12 0", "sa 3 4", "mx 3 7 0", "stt 10 0", "sq 11 1", "add 9",
-    "mx 3 6 1", "st 8", "sa 3 7", "stt 10 1", "tiny1 11", "sa 3 6", "bt 13 0", "tiny2 11", "sq 12 0", "bt 12 1",
-    "stt 11 0", "bt 13 1", "sq 12 1", "add 10", "st 9", "sq 13 1", "stt 11 1", "bt 14 0", "tiny1 12", "sq 13 0",
-    "tiny2 12", "tiny1 13", "sq 14 0", "stt 12 0", "bt 14 1", "add 11", "st 10", "tiny2 13", "sq 14 1", "stt 12 1",
-    "bt 15 0", "tiny1 14", "tiny2 14", "sq 15 0", "stt 13 0", "bt 15 1", "add 12", "st 11", "sq 15 1", "stt 13 1",
-    "tiny1 15", "tiny2 15", "stt 14 0", "add 13", "st 12", "stt 14 1", "stt 15 0", "add 14", "st 13", "stt 15 1",
-    "addh 15 0 G", "st 14", "addh 15 1 V", "sth 15 0", "sth 15 1",
+    "dummy A0", "dummy A1", "gain 1", "vec", "gain 0", "gainS 1", "t x0 C0", "gainS 0", "posT 1", "c x0 V",
+    "posT 0", "posTS 1", "posRC 0", "posTS 0", "t x1 C1", "posRCS 0", "tabT 0 G", "t x2 C0", "c x1 S", "t w0 B0",
+    "c x2 V", "dummy A0", "dummy A1", "t x3 C1", "c w0 V", "tabT 1 G", "t w1 B1", "c x3 S", "t w2 C0", "c w1 S",
+    "dummy A0", "dummy A1", "t w3 C1", "c w2 V", "tabT 2 G", "t w4 B0", "c w3 S", "t w5 B1", "dummy A0", "dummy A1",
+    "t w6 C0", "t w7 C1", "qx 0 0", "qx 0 1", "qw 0", "qw 1", "mx 0 0 1", "qw 2", "c w5 S", "qw 3", "mx 0 1 0",
+    "c w4 V", "tabT 3 G", "sa 0 0", "t x5 B1", "c w6 V", "sa 0 1", "t x4 B0", "c w7 S", "dummy A0", "dummy A1",
+    "t x6 C0", "qw 4", "c x4 S", "qw 5", "t x7 C1", "c x5 S", "qw 6", "qw 7", "mx 0 2 1", "c x6 S", "tabRC 0 V",
+    "mx 0 3 0", "sa 0 2", "t x8 C0", "sa 0 3", "tabRC 1 V", "c x7 S", "mx 0 4 1", "c x8 S", "mx 0 5 0", "sa 0 4",
+    "qx 1 0", "bt 0 0", "bt 1 0", "sa 0 5", "qx 1 1", "t x9 C1", "sq 0 0", "tabT 4 G", "t x10 C0", "c x9 V",
+    "sq 1 0", "mx 0 6 1", "c x10 S", "mx 0 7 0", "sa 0 6", "tabT 5 G", "t x11 C1", "sa 0 7", "t x12 C0", "c x11 S",
+    "bt 0 1", "c x12 S", "bt 1 1", "qx 2 0", "t x13 C1", "sq 0 1", "qx 2 1", "t x14 C0", "sq 1 1", "tabT 6 G",
+    "c x13 V", "mx 1 0 1", "tiny1 0", "c x14 S", "mx 1 1 0", "tiny2 0", "tiny1 1", "sa 1 0", "stt 0 0", "t x15 C1",
+    "tabT 7 G", "tiny2 1", "sa 1 1", "mx 1 2 1", "stt 0 1", "c x15 S", "mx 1 3 0", "sa 1 2", "bt 2 0", "stt 1 0",
+    "sa 1 3", "add 0", "bt 2 1", "mx 1 4 1", "sq 2 1", "mx 1 5 0", "stt 1 1", "sq 2 0", "tiny1 2", "bt 3 0",
+    "sa 1 4", "tiny2 2", "bt 3 1", "add 1", "sa 1 5", "st 0", "stt 2 0", "mx 1 6 1", "sq 3 1", "mx 1 7 0",
+    "sq 3 0", "stt 2 1", "tiny1 3", "sa 1 6", "tiny2 3", "qx 3 0", "st 1", "sa 1 7", "add 2", "stt 3 0", "stt 3 1",
+    "qx 3 1", "st 2", "add 3", "st 3", "bt 4 1", "bt 4 0", "sq 4 1", "sq 4 0", "tiny1 4", "mx 2 0 1", "sa 2 0",
+    "tiny2 4", "mx 2 1 0", "sa 2 1", "stt 4 0", "stt 4 1", "add 4", "st 4", "bt 5 1", "bt 5 0", "sq 5 1", "sq 5 0",
+    "tiny1 5", "mx 2 2 1", "sa 2 2", "tiny2 5", "mx 2 3 0", "sa 2 3", "stt 5 0", "stt 5 1", "add 5", "st 5",
+    "bt 6 1", "bt 6 0", "sq 6 1", "sq 6 0", "tiny1 6", "mx 2 4 1", "sa 2 4", "tiny2 6", "mx 2 5 0", "sa 2 5",
+    "stt 6 0", "stt 6 1", "add 6", "st 6", "bt 7 1", "bt 7 0", "sq 7 1", "sq 7 0", "tiny1 7", "mx 2 6 1", "sa 2 6",
+    "tiny2 7", "mx 2 7 0", "sa 2 7", "stt 7 0", "stt 7 1", "add 7", "st 7", "bt 8 1", "bt 8 0", "sq 8 1", "sq 8 0",
+    "tiny1 8", "mx 3 0 1", "sa 3 0", "tiny2 8", "mx 3 1 0", "sa 3 1", "stt 8 0", "stt 8 1", "add 8", "st 8",
+    "bt 9 1", "bt 9 0", "sq 9 1", "sq 9 0", "tiny1 9", "mx 3 2 1", "sa 3 2", "tiny2 9", "mx 3 3 0", "sa 3 3",
+    "stt 9 0", "stt 9 1", "add 9", "st 9", "bt 10 1", "bt 10 0", "sq 10 1", "sq 10 0", "tiny1 10", "mx 3 4 1",
+    "sa 3 4", "tiny2 10", "mx 3 5 0", "sa 3 5", "stt 10 0", "stt 10 1", "add 10", "st 10", "bt 11 1", "bt 11 0",
+    "sq 11 1", "sq 11 0", "tiny1 11", "mx 3 6 1", "sa 3 6", "tiny2 11", "mx 3 7 0", "sa 3 7", "stt 11 0", "stt 11 1",
+    "add 11", "st 11", "bt 12 1", "bt 12 0", "sq 12 1", "sq 12 0", "tiny1 12", "tiny2 12", "stt 12 0", "stt 12 1",
+    "add 12", "st 12", "bt 13 1", "bt 13 0", "sq 13 1", "sq 13 0", "tiny1 13", "tiny2 13", "stt 13 0", "stt 13 1",
+    "add 13", "st 13", "bt 14 1", "bt 14 0", "sq 14 1", "sq 14 0", "tiny1 14", "tiny2 14", "stt 14 0", "addh 14 0 G",
+    "sth 14 0", "stt 14 1", "addh 14 1 V", "sth 14 1", "bt 15 1", "bt 15 0", "sq 15 1", "sq 15 0", "tiny1 15",
+    "tiny2 15", "stt 15 0", "addh 15 0 G", "sth 15 0", "stt 15 1", "addh 15 1 V", "sth 15 1",
 )
 
 
@@ -86,6 +87,8 @@ def tile_causalwanselfattention_pa_kernel(tc, x, W, b, g, freqs_cos, freqs_sin, 
         nc.vector.memset(warm[:], 1.0)
         ones_b = const.tile([P, P], BF16, name="ones_b")
         nc.vector.memset(ones_b[:], 1.0)
+        wide = const.tile([P, 512], BF16, name="wide")
+        nc.vector.memset(wide[:], 1.0)
         nc.scalar.dma_start(out=fsrc[0:16, 0:64], in_=freqs_cos)
         nc.scalar.dma_start(out=fsrc[0:16, 64:128], in_=freqs_sin)
         nc.sync.dma_start(out=fsrc[0:8, 256:384], in_=g.rearrange("(h d) -> h d", d=P))
@@ -128,6 +131,10 @@ def tile_causalwanselfattention_pa_kernel(tc, x, W, b, g, freqs_cos, freqs_sin, 
         tab_rc = const.tile([P, 2, 2, NH, DRC], F32, name="tab_rc")
 
         live = {}
+
+        def op_dummy(tag):
+            ps_w = psum.tile([P, 512], F32, tag=tag, name="ps_w")
+            nc.tensor.matmul(out=ps_w[:], lhsT=ones_b[:], rhs=wide[:], start=True, stop=True)
 
         def op_gain(half):
             half = int(half)
@@ -345,7 +352,7 @@ def tile_causalwanselfattention_pa_kernel(tc, x, W, b, g, freqs_cos, freqs_sin, 
             nc.sync.dma_start(out=out_rows[P * i : P * (i + 1), cols], in_=live[("o", i)][:, cols])
 
         ops = {
-            "gain": op_gain, "gainS": op_gainS, "vec": op_vec, "posT": op_posT, "posTS": op_posTS, "posRC": op_posRC,
+            "dummy": op_dummy, "gain": op_gain, "gainS": op_gainS, "vec": op_vec, "posT": op_posT, "posTS": op_posTS, "posRC": op_posRC,
             "posRCS": op_posRCS, "tabT": op_tabT, "tabRC": op_tabRC, "t": op_t, "c": op_c, "qx": op_qx, "qw": op_qw,
             "mx": op_mx, "sa": op_sa, "bt": op_bt, "sq": op_sq, "tiny1": op_tiny1, "tiny2": op_tiny2, "stt": op_stt,
             "add": op_add, "st": op_st, "addh": op_addh, "sth": op_sth,

@@ -15,46 +15,22 @@ ALU = mybir.AluOpType
 
 P = 128
 K = 1024
-NH = 8
-NCH = 4
+PASSES = 2
+HEADS = 8
+HEAD = 128
+FEATURES = HEADS * HEAD
+CHUNK = 512
+CHUNKS = 4
+TILES = 16
+FRAMES = 8
+FRAME_PART = 44
+GRID_PART = HEAD - FRAME_PART
+ROW_PART = 42
 EPS = 1e-6
-DT2 = 44
-DRC = 84
-SLOTS = ("A", "B", "A", "B", "A", "B", "A", "B", "C", "A", "B", "C", "A", "B", "C", "A")
-ORDER = (
-    "dummy A0", "dummy A1", "gain 1", "vec", "gain 0", "gainS 1", "t x0 C0", "gainS 0", "posT 1", "c x0 V",
-    "posT 0", "posTS 1", "posRC 0", "posTS 0", "t x1 C1", "posRCS 0", "tabT 0 G", "t x2 C0", "c x1 S", "t w0 B0",
-    "c x2 V", "dummy A0", "dummy A1", "t x3 C1", "c w0 V", "tabT 1 G", "t w1 B1", "c x3 S", "t w2 C0", "c w1 S",
-    "dummy A0", "dummy A1", "t w3 C1", "c w2 V", "tabT 2 G", "t w4 B0", "c w3 S", "t w5 B1", "dummy A0", "dummy A1",
-    "t w6 C0", "t w7 C1", "qx 0 0", "qx 0 1", "qw 0", "qw 1", "mx 0 0 1", "qw 2", "c w5 S", "qw 3", "mx 0 1 0",
-    "c w4 V", "tabT 3 G", "sa 0 0", "t x5 B1", "c w6 V", "sa 0 1", "t x4 B0", "c w7 S", "dummy A0", "dummy A1",
-    "t x6 C0", "qw 4", "c x4 S", "qw 5", "t x7 C1", "c x5 S", "qw 6", "qw 7", "mx 0 2 1", "c x6 S", "tabRC 0 V",
-    "mx 0 3 0", "sa 0 2", "t x8 C0", "sa 0 3", "tabRC 1 V", "c x7 S", "mx 0 4 1", "c x8 S", "mx 0 5 0", "sa 0 4",
-    "qx 1 0", "bt 0 0", "bt 1 0", "sa 0 5", "qx 1 1", "t x9 C1", "sq 0 0", "tabT 4 G", "t x10 C0", "c x9 V",
-    "sq 1 0", "mx 0 6 1", "c x10 S", "mx 0 7 0", "sa 0 6", "tabT 5 G", "t x11 C1", "sa 0 7", "t x12 C0", "c x11 S",
-    "bt 0 1", "c x12 S", "bt 1 1", "qx 2 0", "t x13 C1", "sq 0 1", "qx 2 1", "t x14 C0", "sq 1 1", "tabT 6 G",
-    "c x13 V", "mx 1 0 1", "tiny1 0", "c x14 S", "mx 1 1 0", "tiny2 0", "tiny1 1", "sa 1 0", "stt 0 0", "t x15 C1",
-    "tabT 7 G", "tiny2 1", "sa 1 1", "mx 1 2 1", "stt 0 1", "c x15 S", "mx 1 3 0", "sa 1 2", "bt 2 0", "stt 1 0",
-    "sa 1 3", "add 0", "bt 2 1", "mx 1 4 1", "sq 2 1", "mx 1 5 0", "stt 1 1", "sq 2 0", "tiny1 2", "bt 3 0",
-    "sa 1 4", "tiny2 2", "bt 3 1", "add 1", "sa 1 5", "st 0", "stt 2 0", "mx 1 6 1", "sq 3 1", "mx 1 7 0",
-    "sq 3 0", "stt 2 1", "tiny1 3", "sa 1 6", "tiny2 3", "qx 3 0", "st 1", "sa 1 7", "add 2", "stt 3 0", "stt 3 1",
-    "qx 3 1", "st 2", "add 3", "st 3", "bt 4 1", "bt 4 0", "sq 4 1", "sq 4 0", "tiny1 4", "mx 2 0 1", "sa 2 0",
-    "tiny2 4", "mx 2 1 0", "sa 2 1", "stt 4 0", "stt 4 1", "add 4", "st 4", "bt 5 1", "bt 5 0", "sq 5 1", "sq 5 0",
-    "tiny1 5", "mx 2 2 1", "sa 2 2", "tiny2 5", "mx 2 3 0", "sa 2 3", "stt 5 0", "stt 5 1", "add 5", "st 5",
-    "bt 6 1", "bt 6 0", "sq 6 1", "sq 6 0", "tiny1 6", "mx 2 4 1", "sa 2 4", "tiny2 6", "mx 2 5 0", "sa 2 5",
-    "stt 6 0", "stt 6 1", "add 6", "st 6", "bt 7 1", "bt 7 0", "sq 7 1", "sq 7 0", "tiny1 7", "mx 2 6 1", "sa 2 6",
-    "tiny2 7", "mx 2 7 0", "sa 2 7", "stt 7 0", "stt 7 1", "add 7", "st 7", "bt 8 1", "bt 8 0", "sq 8 1", "sq 8 0",
-    "tiny1 8", "mx 3 0 1", "sa 3 0", "tiny2 8", "mx 3 1 0", "sa 3 1", "stt 8 0", "stt 8 1", "add 8", "st 8",
-    "bt 9 1", "bt 9 0", "sq 9 1", "sq 9 0", "tiny1 9", "mx 3 2 1", "sa 3 2", "tiny2 9", "mx 3 3 0", "sa 3 3",
-    "stt 9 0", "stt 9 1", "add 9", "st 9", "bt 10 1", "bt 10 0", "sq 10 1", "sq 10 0", "tiny1 10", "mx 3 4 1",
-    "sa 3 4", "tiny2 10", "mx 3 5 0", "sa 3 5", "stt 10 0", "stt 10 1", "add 10", "st 10", "bt 11 1", "bt 11 0",
-    "sq 11 1", "sq 11 0", "tiny1 11", "mx 3 6 1", "sa 3 6", "tiny2 11", "mx 3 7 0", "sa 3 7", "stt 11 0", "stt 11 1",
-    "add 11", "st 11", "bt 12 1", "bt 12 0", "sq 12 1", "sq 12 0", "tiny1 12", "tiny2 12", "stt 12 0", "stt 12 1",
-    "add 12", "st 12", "bt 13 1", "bt 13 0", "sq 13 1", "sq 13 0", "tiny1 13", "tiny2 13", "stt 13 0", "stt 13 1",
-    "add 13", "st 13", "bt 14 1", "bt 14 0", "sq 14 1", "sq 14 0", "tiny1 14", "tiny2 14", "stt 14 0", "addh 14 0 G",
-    "sth 14 0", "stt 14 1", "addh 14 1 V", "sth 14 1", "bt 15 1", "bt 15 0", "sq 15 1", "sq 15 0", "tiny1 15",
-    "tiny2 15", "stt 15 0", "addh 15 0 G", "sth 15 0", "stt 15 1", "addh 15 1 V", "sth 15 1",
-)
+
+VECTOR_COPIES = ("x0", "x2", "w0", "w2", "w4", "w6", "x9", "x13")
+GPSIMD_FRAME_TABLES = 5
+FIRST_SHARED_ADD = 14
 
 
 def tile_causalwanselfattention_pa_kernel(tc, x, W, b, g, freqs_cos, freqs_sin, out):
@@ -64,299 +40,348 @@ def tile_causalwanselfattention_pa_kernel(tc, x, W, b, g, freqs_cos, freqs_sin, 
 
     with ExitStack() as ctx:
         const = ctx.enter_context(tc.tile_pool(name="const", bufs=1))
-        rawp = ctx.enter_context(tc.tile_pool(name="rawp", bufs=24))
-        grp = ctx.enter_context(tc.tile_pool(name="grp", bufs=2))
+        inputs = ctx.enter_context(tc.tile_pool(name="inputs", bufs=24))
+        grouped = ctx.enter_context(tc.tile_pool(name="grouped", bufs=2))
         ypool = ctx.enter_context(tc.tile_pool(name="ypool", bufs=2))
         work = ctx.enter_context(tc.tile_pool(name="work", bufs=4))
         small = ctx.enter_context(tc.tile_pool(name="small", bufs=4))
         psum = ctx.enter_context(tc.psum_pool(name="psum", bufs=1))
         ctx.enter_context(tc.manual_schedule())
 
-        def eng_of(name):
-            return {"V": nc.vector, "G": nc.gpsimd, "S": nc.scalar}[name]
+        rows = const.tile([P, 384], BF16, name="rows")
+        nc.vector.memset(rows[:], 0.0)
+        one = const.tile([P, 2], F32, name="one")
+        nc.vector.memset(one[:], 1.0)
+        ones = const.tile([P, P], BF16, name="ones")
+        nc.vector.memset(ones[:], 1.0)
+        ones_wide = const.tile([P, CHUNK], BF16, name="ones_wide")
+        nc.vector.memset(ones_wide[:], 1.0)
+        nc.scalar.dma_start(out=rows[0:16, 0:64], in_=freqs_cos)
+        nc.scalar.dma_start(out=rows[0:16, 64:128], in_=freqs_sin)
+        nc.sync.dma_start(out=rows[0:HEADS, 256:384], in_=g.rearrange("(h d) -> h d", d=HEAD))
+        nc.sync.dma_start(out=rows[0:HEADS, 128:256], in_=b.rearrange("(h d) -> h d", d=HEAD))
 
-        def copy_on(name, dst, srcv):
-            if name == "S":
-                nc.scalar.copy(out=dst, in_=srcv)
+        raw = {}
+        for name in ["x%d" % t for t in range(4)] + ["w%d" % h for h in range(HEADS)] + ["x%d" % t for t in range(4, TILES)]:
+            n = int(name[1:])
+            raw[name] = inputs.tile([P, K], BF16, tag="raw", name="raw_" + name)
+            source = x_rows if name[0] == "x" else W
+            nc.sync.dma_start(out=raw[name][:], in_=source[P * n : P * (n + 1), :])
+
+        ident_bf = const.tile([P, P], BF16, name="ident_bf")
+        make_identity(nc, ident_bf[:])
+        ident = const.tile([P, P], F32, name="ident")
+        make_identity(nc, ident[:])
+        nc.scalar.activation(out=one[:, 1:2], in_=one[:, 0:1], func=ACT.Abs_reciprocal_sqrt)
+
+        w_codes = const.tile([P, HEADS, PASSES, HEAD], U32, name="w_codes", align_bytes=64)
+        w_scales = const.tile([P, HEADS, PASSES, HEAD], U8, name="w_scales", align_bytes=64)
+        x_codes = const.tile([P, CHUNKS, PASSES, CHUNK], U32, name="x_codes", align_bytes=64)
+        x_scales = const.tile([P, CHUNKS, PASSES, CHUNK], U8, name="x_scales", align_bytes=64)
+        gain = const.tile([P, FEATURES], F32, name="gain")
+        gain_heads = gain.rearrange("p (h d) -> p h d", d=HEAD)
+        bias = const.tile([P, HEADS], F32, name="bias")
+        frame_pos = const.tile([P, 2, FRAMES, FRAME_PART], F32, name="frame_pos")
+        grid_pos = const.tile([P, 2, 2, GRID_PART], F32, name="grid_pos")
+        frame_table = const.tile([P, FRAMES, 2, HEADS, FRAME_PART], F32, name="frame_table")
+        grid_table = const.tile([P, 2, 2, HEADS, GRID_PART], F32, name="grid_table")
+        freq = const.tile([P, 2, HEAD], BF16, name="freq")
+        freq_by_frame = const.tile([P, 2, FRAMES, FRAME_PART], BF16, name="freq_by_frame")
+        pick_row = const.tile([P, 2, P], BF16, name="pick_row")
+        pick_column = const.tile([P, P], BF16, name="pick_column")
+
+        banks = {}
+        tiles = {}
+
+        def empty_bank(on_vector, dst, src):
+            if on_vector:
+                nc.vector.tensor_copy(out=dst, in_=src)
             else:
-                nc.vector.tensor_copy(out=dst, in_=srcv)
+                nc.scalar.copy(out=dst, in_=src)
 
-        fsrc = const.tile([P, 384], BF16, name="fsrc")
-        nc.vector.memset(fsrc[:], 0.0)
-        warm = const.tile([P, 2], F32, name="warm")
-        nc.vector.memset(warm[:], 1.0)
-        ones_b = const.tile([P, P], BF16, name="ones_b")
-        nc.vector.memset(ones_b[:], 1.0)
-        wide = const.tile([P, 512], BF16, name="wide")
-        nc.vector.memset(wide[:], 1.0)
-        nc.scalar.dma_start(out=fsrc[0:16, 0:64], in_=freqs_cos)
-        nc.scalar.dma_start(out=fsrc[0:16, 64:128], in_=freqs_sin)
-        nc.sync.dma_start(out=fsrc[0:8, 256:384], in_=g.rearrange("(h d) -> h d", d=P))
-        nc.sync.dma_start(out=fsrc[0:8, 128:256], in_=b.rearrange("(h d) -> h d", d=P))
+        def idle_matmuls():
+            for bank in ("a0", "a1"):
+                unused = psum.tile([P, CHUNK], F32, tag=bank, name="unused")
+                nc.tensor.matmul(out=unused[:], lhsT=ones[:], rhs=ones_wide[:], start=True, stop=True)
 
-        raw_tiles = {}
-
-        def load(key, rows):
-            t = rawp.tile([P, K], BF16, tag="raw", name="raw_" + key)
-            nc.sync.dma_start(out=t[:], in_=rows)
-            raw_tiles[key] = t
-
-        for t in range(4):
-            load("x%d" % t, x_rows[P * t : P * (t + 1), :])
-        for h in range(NH):
-            load("w%d" % h, W[P * h : P * (h + 1), :])
-        for t in range(4, 16):
-            load("x%d" % t, x_rows[P * t : P * (t + 1), :])
-
-        ident_b = const.tile([P, P], BF16, name="ident_b")
-        make_identity(nc, ident_b[:])
-        ident_f = const.tile([P, P], F32, name="ident_f")
-        make_identity(nc, ident_f[:])
-        nc.scalar.activation(out=warm[:, 1:2], in_=warm[:, 0:1], func=ACT.Abs_reciprocal_sqrt)
-
-        wc = const.tile([P, NH, 2, P], U32, name="wc", align_bytes=64)
-        ws = const.tile([P, NH, 2, P], U8, name="ws", align_bytes=64)
-        xc = const.tile([P, NCH, 2, 512], U32, name="xc", align_bytes=64)
-        xs = const.tile([P, NCH, 2, 512], U8, name="xs", align_bytes=64)
-        g_b = const.tile([P, K], F32, name="g_b")
-        pos_t = const.tile([P, 2, 8, DT2], F32, name="pos_t")
-        pos_rc = const.tile([P, 2, 2, DRC], F32, name="pos_rc")
-        b_col = const.tile([P, NH], F32, name="b_col")
-        fe = const.tile([P, 2, P], BF16, name="fe")
-        x_t = const.tile([P, 2, 8, DT2], BF16, name="x_t")
-        selr = const.tile([P, 2, P], BF16, name="selr")
-        selc = const.tile([P, P], BF16, name="selc")
-        g_b3 = g_b.rearrange("p (h d) -> p h d", d=P)
-        tab_t = const.tile([P, 8, 2, NH, DT2], F32, name="tab_t")
-        tab_rc = const.tile([P, 2, 2, NH, DRC], F32, name="tab_rc")
-
-        live = {}
-
-        def op_dummy(tag):
-            ps_w = psum.tile([P, 512], F32, tag=tag, name="ps_w")
-            nc.tensor.matmul(out=ps_w[:], lhsT=ones_b[:], rhs=wide[:], start=True, stop=True)
-
-        def op_gain(half):
-            half = int(half)
-            ps_g = psum.tile([P, 512], F32, tag="A%d" % half, name="ps_g")
-            for hh in range(4):
-                h = 4 * half + hh
+        def spread_gain(half):
+            spread = psum.tile([P, CHUNK], F32, tag="a%d" % half, name="spread")
+            for i in range(4):
+                h = 4 * half + i
                 nc.tensor.matmul(
-                    out=ps_g[:, P * hh : P * (hh + 1)], lhsT=ident_b[:, h : h + 1].to_broadcast([P, P]),
-                    rhs=fsrc[:, 256:384], start=True, stop=True,
+                    out=spread[:, HEAD * i : HEAD * (i + 1)], lhsT=ident_bf[:, h : h + 1].to_broadcast([P, P]),
+                    rhs=rows[:, 256:384], start=True, stop=True,
                 )
-            live[("g", half)] = ps_g
+            nc.scalar.copy(out=gain[:, CHUNK * half : CHUNK * (half + 1)], in_=spread[:])
 
-        def op_gainS(half, eng="S"):
-            half = int(half)
-            copy_on(eng, g_b[:, 512 * half : 512 * (half + 1)], live[("g", half)][:])
-
-        def op_vec():
+        def prepare_selection():
             nc.vector.tensor_copy(
-                out=fe.rearrange("p c (j e) -> p (c j) e", e=2), in_=fsrc[:, 0:128].unsqueeze(2).to_broadcast([P, P, 2])
+                out=freq.rearrange("p c (j e) -> p (c j) e", e=2), in_=rows[:, 0:128].unsqueeze(2).to_broadcast([P, P, 2])
             )
             nc.vector.tensor_copy(
-                out=selr.rearrange("p a (b c) -> p (a b) c", c=16),
-                in_=ident_b[:, 0:16].unsqueeze(2).to_broadcast([P, 16, 16]),
+                out=pick_row.rearrange("p a (b c) -> p (a b) c", c=16),
+                in_=ident_bf[:, 0:16].unsqueeze(2).to_broadcast([P, 16, 16]),
             )
-            sin_odd = fe.rearrange("p c (j e) -> p c j e", e=2)[:, 1, :, 1:2]
+            sin_odd = freq.rearrange("p c (j e) -> p c j e", e=2)[:, 1, :, 1:2]
             nc.vector.tensor_scalar_mul(out=sin_odd, in0=sin_odd, scalar1=-1.0)
             nc.vector.tensor_copy(
-                out=selc.rearrange("p (a c) -> p a c", c=16), in_=ident_b[:, 0:16].unsqueeze(1).to_broadcast([P, 8, 16])
+                out=pick_column.rearrange("p (a c) -> p a c", c=16),
+                in_=ident_bf[:, 0:16].unsqueeze(1).to_broadcast([P, 8, 16]),
             )
             nc.vector.tensor_tensor(
-                out=x_t[:],
-                in0=fe[:, :, 0:DT2].unsqueeze(2).to_broadcast([P, 2, 8, DT2]),
-                in1=ident_b[:, 0:8].unsqueeze(1).unsqueeze(3).to_broadcast([P, 2, 8, DT2]),
+                out=freq_by_frame[:],
+                in0=freq[:, :, 0:FRAME_PART].unsqueeze(2).to_broadcast([P, 2, FRAMES, FRAME_PART]),
+                in1=ident_bf[:, 0:FRAMES].unsqueeze(1).unsqueeze(3).to_broadcast([P, 2, FRAMES, FRAME_PART]),
                 op=ALU.mult,
             )
 
-        def op_posT(cs):
-            cs = int(cs)
-            ps_t = psum.tile([P, 512], F32, tag="B%d" % cs, name="ps_t")
+        def spread_frame_positions(cs):
+            spread = psum.tile([P, CHUNK], F32, tag="b%d" % cs, name="spread")
+            width = FRAMES * FRAME_PART
             nc.tensor.matmul(
-                out=ps_t[:, 0:352], lhsT=ones_b[:], rhs=x_t[:, cs].rearrange("p f d -> p (f d)"), start=True, stop=True
+                out=spread[:, 0:width], lhsT=ones[:], rhs=freq_by_frame[:, cs].rearrange("p f d -> p (f d)"),
+                start=True, stop=True,
             )
-            live[("pt", cs)] = ps_t
+            nc.scalar.copy(out=frame_pos[:, cs].rearrange("p f d -> p (f d)"), in_=spread[:, 0:width])
 
-        def op_posTS(cs, eng="S"):
-            cs = int(cs)
-            copy_on(eng, pos_t[:, cs].rearrange("p f d -> p (f d)"), live[("pt", cs)][:, 0:352])
-
-        def op_posRC(k):
-            ps_e = psum.tile([P, 512], F32, tag="acc" + k, name="ps_e")
-            for par in range(2):
+        def pick_grid_positions_and_bias():
+            picked = psum.tile([P, CHUNK], F32, tag="mx0", name="picked")
+            for parity in range(2):
                 for cs in range(2):
-                    o0 = DRC * (2 * par + cs)
+                    at = GRID_PART * (2 * parity + cs)
                     nc.tensor.matmul(
-                        out=ps_e[:, o0 : o0 + 42], lhsT=selr[:, par, :], rhs=fe[:, cs, 44:86], start=True, stop=True
+                        out=picked[:, at : at + ROW_PART], lhsT=pick_row[:, parity, :],
+                        rhs=freq[:, cs, FRAME_PART : FRAME_PART + ROW_PART], start=True, stop=True,
                     )
                     nc.tensor.matmul(
-                        out=ps_e[:, o0 + 42 : o0 + 84], lhsT=selc[:], rhs=fe[:, cs, 86:128], start=True, stop=True
+                        out=picked[:, at + ROW_PART : at + GRID_PART], lhsT=pick_column[:],
+                        rhs=freq[:, cs, FRAME_PART + ROW_PART : HEAD], start=True, stop=True,
                     )
-            nc.tensor.matmul(out=ps_e[:, 336:344], lhsT=fsrc[:, 128:256], rhs=ident_b[:, 0:8], start=True, stop=True)
-            live["pe"] = ps_e
+            width = 4 * GRID_PART
+            nc.tensor.matmul(
+                out=picked[:, width : width + HEADS], lhsT=rows[:, 128:256], rhs=ident_bf[:, 0:HEADS], start=True, stop=True
+            )
+            nc.scalar.copy(out=bias[:], in_=picked[:, width : width + HEADS])
+            nc.scalar.copy(out=grid_pos.rearrange("p a c n -> p (a c n)"), in_=picked[:, 0:width])
 
-        def op_posRCS(k, eng="S"):
-            copy_on(eng, b_col[:], live["pe"][:, 336:344])
-            copy_on(eng, pos_rc.rearrange("p a c n -> p (a c n)"), live["pe"][:, 0:336])
-
-        def op_tabT(f, eng="G"):
-            f = int(f)
-            eng_of(eng).tensor_tensor(
-                out=tab_t[:, f],
-                in0=g_b3[:, :, 0:DT2].unsqueeze(1).to_broadcast([P, 2, NH, DT2]),
-                in1=pos_t[:, :, f, :].unsqueeze(2).to_broadcast([P, 2, NH, DT2]),
+        def build_frame_table(engine, frame):
+            shape = [P, 2, HEADS, FRAME_PART]
+            engine.tensor_tensor(
+                out=frame_table[:, frame],
+                in0=gain_heads[:, :, 0:FRAME_PART].unsqueeze(1).to_broadcast(shape),
+                in1=frame_pos[:, :, frame, :].unsqueeze(2).to_broadcast(shape),
                 op=ALU.mult,
             )
 
-        def op_tabRC(par, eng="V"):
-            par = int(par)
-            eng_of(eng).tensor_tensor(
-                out=tab_rc[:, par],
-                in0=g_b3[:, :, DT2:P].unsqueeze(1).to_broadcast([P, 2, NH, DRC]),
-                in1=pos_rc[:, par].unsqueeze(2).to_broadcast([P, 2, NH, DRC]),
+        def build_grid_table(parity):
+            shape = [P, 2, HEADS, GRID_PART]
+            nc.vector.tensor_tensor(
+                out=grid_table[:, parity],
+                in0=gain_heads[:, :, FRAME_PART:HEAD].unsqueeze(1).to_broadcast(shape),
+                in1=grid_pos[:, parity].unsqueeze(2).to_broadcast(shape),
                 op=ALU.mult,
             )
 
-        def op_t(key, tag):
-            words = raw_tiles[key].bitcast(F32)
-            xt = psum.tile([P, 2, 2, P], F32, tag=tag, name="xt_" + key)
-            for gi in range(2):
+        def bring_in(name, bank):
+            words = raw[name].bitcast(F32)
+            turned = psum.tile([P, PASSES, 2, P], F32, tag=bank, name="turned_" + name)
+            for gi in range(PASSES):
                 for u in range(2):
-                    nc.tensor.transpose(xt[:, gi, u, :], words[:, 256 * gi + u : 256 * (gi + 1) : 2], ident_f[:])
-            live[("xt", key)] = xt
-
-        def op_c(key, eng):
-            n = int(key[1:])
-            if key[0] == "x":
-                c, tt = divmod(n, 4)
-                if ("xg", c) not in live:
-                    live[("xg", c)] = grp.tile([P, 2, 2048], BF16, tag="xg", name="xg", align_bytes=64)
-                dst = live[("xg", c)].bitcast(F32)[:, :, 256 * tt : 256 * (tt + 1)]
+                    nc.tensor.transpose(turned[:, gi, u, :], words[:, 256 * gi + u : 256 * (gi + 1) : 2], ident[:])
+            n = int(name[1:])
+            if name[0] == "x":
+                chunk, place = divmod(n, 4)
+                if place == 0:
+                    tiles[("x", chunk)] = grouped.tile([P, PASSES, 4 * CHUNK], BF16, tag="xg", name="xg", align_bytes=64)
+                dst = tiles[("x", chunk)].bitcast(F32)[:, :, 256 * place : 256 * (place + 1)]
             else:
-                live[("wg", n)] = grp.tile([P, 2, 512], BF16, tag="wg", name="wg", align_bytes=64, bufs=4)
-                dst = live[("wg", n)].bitcast(F32)
-            copy_on(eng, dst.rearrange("p g (r u) -> p g r u", u=2), live[("xt", key)].rearrange("p g u r -> p g r u"))
-
-        def op_qx(c, gi):
-            c, gi = int(c), int(gi)
-            nc.vector.quantize_mx(
-                out=xc[:, c, gi, :].bitcast(FP8X4), scales=xs[:, c, gi, :], in_=live[("xg", c)][:, gi, :]
+                tiles[("w", n)] = grouped.tile([P, PASSES, 4 * HEAD], BF16, tag="wg", name="wg", align_bytes=64, bufs=4)
+                dst = tiles[("w", n)].bitcast(F32)
+            empty_bank(
+                name in VECTOR_COPIES, dst.rearrange("p g (r u) -> p g r u", u=2), turned.rearrange("p g u r -> p g r u")
             )
 
-        def op_qw(h):
-            h = int(h)
+        def quantize_x(chunk, gi):
             nc.vector.quantize_mx(
-                out=wc[:, h].rearrange("p g m -> p (g m)").bitcast(FP8X4),
-                scales=ws[:, h].rearrange("p g m -> p (g m)"),
-                in_=live[("wg", h)].rearrange("p g n -> p (g n)"),
+                out=x_codes[:, chunk, gi, :].bitcast(FP8X4), scales=x_scales[:, chunk, gi, :],
+                in_=tiles[("x", chunk)][:, gi, :],
             )
 
-        def op_mx(c, h, k):
-            c, h = int(c), int(h)
-            acc = psum.tile([P, 512], F32, tag="acc" + k, name="acc")
-            for gi in range(2):
+        def quantize_w(head):
+            nc.vector.quantize_mx(
+                out=w_codes[:, head].rearrange("p g m -> p (g m)").bitcast(FP8X4),
+                scales=w_scales[:, head].rearrange("p g m -> p (g m)"),
+                in_=tiles[("w", head)].rearrange("p g n -> p (g n)"),
+            )
+
+        def project(chunk, head):
+            acc = psum.tile([P, CHUNK], F32, tag="mx%d" % ((head + 1) % 2), name="acc")
+            for gi in range(PASSES):
                 nc.tensor.matmul_mx(
                     out=acc[:],
-                    lhsT=wc[:, h, gi, :].bitcast(FP8X4),
-                    lhsT_scale=ws[:, h, gi, :],
-                    rhs=xc[:, c, gi, :].bitcast(FP8X4),
-                    rhs_scale=xs[:, c, gi, :],
+                    lhsT=w_codes[:, head, gi, :].bitcast(FP8X4),
+                    lhsT_scale=w_scales[:, head, gi, :],
+                    rhs=x_codes[:, chunk, gi, :].bitcast(FP8X4),
+                    rhs_scale=x_scales[:, chunk, gi, :],
                     start=(gi == 0),
-                    stop=(gi == 1),
+                    stop=(gi == PASSES - 1),
                 )
-            live[("acc", c, h)] = acc
-
-        def op_sa(c, h):
-            c, h = int(c), int(h)
-            if ("ysb", c) not in live:
-                live[("ysb", c)] = ypool.tile([P, NH, 512], F32, tag="ysb", name="ysb")
+            if head == 0:
+                tiles[("y", chunk)] = ypool.tile([P, HEADS, CHUNK], F32, tag="y", name="y")
             nc.scalar.activation(
-                out=live[("ysb", c)][:, h, :], in_=live[("acc", c, h)][:], func=ACT.Identity,
-                bias=b_col[:, h : h + 1], scale=1.0,
+                out=tiles[("y", chunk)][:, head, :], in_=acc[:], func=ACT.Identity, bias=bias[:, head : head + 1], scale=1.0
             )
 
-        def op_bt(i, bk):
-            i, bk = int(i), int(bk)
-            c, tt = divmod(i, 4)
-            yt = psum.tile([P, 512], F32, tag="%s%d" % (SLOTS[i], bk), name="yT%d" % bk)
-            for hh in range(4):
+        def turn_back(t, half):
+            chunk, place = divmod(t, 4)
+            y_tokens = psum.tile([P, CHUNK], F32, tag="%s%d" % ("abc"[t % 3], half), name="y_tokens")
+            for i in range(4):
                 nc.tensor.transpose(
-                    yt[:, P * hh : P * (hh + 1)], live[("ysb", c)][:, 4 * bk + hh, P * tt : P * (tt + 1)], ident_f[:]
+                    y_tokens[:, HEAD * i : HEAD * (i + 1)],
+                    tiles[("y", chunk)][:, 4 * half + i, P * place : P * (place + 1)], ident[:],
                 )
-            live[("yt", i, bk)] = yt
-
-        def op_sq(i, bk):
-            i, bk = int(i), int(bk)
-            if ("ss", i) not in live:
-                live[("ss", i)] = small.tile([P, 4], F32, tag="ss", name="ss")
-            junk = work.tile([P, 512], F32, tag="junk", name="junk", bufs=2)
+            banks[(t, half)] = y_tokens
+            if ("stats", t) not in tiles:
+                tiles[("stats", t)] = small.tile([P, 4], F32, tag="stats", name="stats")
+            squares = work.tile([P, CHUNK], F32, tag="squares", name="squares", bufs=2)
             nc.scalar.activation(
-                out=junk[:], in_=live[("yt", i, bk)][:], func=ACT.Square, scale=0.03125,
-                accum_out=live[("ss", i)][:, bk : bk + 1],
+                out=squares[:], in_=y_tokens[:], func=ACT.Square, scale=0.03125,
+                accum_out=tiles[("stats", t)][:, half : half + 1],
             )
 
-        def op_tiny1(i):
-            ss = live[("ss", int(i))]
-            nc.scalar.activation(out=ss[:, 2:3], in_=ss[:, 1:2], func=ACT.Identity, bias=EPS, scale=1.0)
+        def add_eps(t):
+            stats = tiles[("stats", t)]
+            nc.scalar.activation(out=stats[:, 2:3], in_=stats[:, 1:2], func=ACT.Identity, bias=EPS, scale=1.0)
 
-        def op_tiny2(i):
-            ss = live[("ss", int(i))]
+        def take_rstd(t):
+            stats = tiles[("stats", t)]
             nc.scalar.activation(
-                out=ss[:, 3:4], in_=ss[:, 0:1], func=ACT.Abs_reciprocal_sqrt, bias=ss[:, 2:3], scale=1.0
+                out=stats[:, 3:4], in_=stats[:, 0:1], func=ACT.Abs_reciprocal_sqrt, bias=stats[:, 2:3], scale=1.0
             )
 
-        def op_stt(i, bk):
-            i, bk = int(i), int(bk)
-            f, par = divmod(i, 2)
-            if ("t", i) not in live:
-                t1 = work.tile([P, NH, P], F32, tag="t1", name="t1")
-                t2 = work.tile([P, NH, P], F32, tag="t2", name="t2")
-                live[("t", i)] = (t1, t2)
-            y3 = live[("yt", i, bk)].rearrange("p (h d) -> p h d", d=P)
-            hs = slice(4 * bk, 4 * bk + 4)
-            for cs in range(2):
-                dst = live[("t", i)][cs]
-                for lo, hi, tab in ((0, DT2, tab_t[:, f, cs, hs, :]), (DT2, P, tab_rc[:, par, cs, hs, :])):
-                    nc.vector.scalar_tensor_tensor(
-                        out=dst[:, hs, lo:hi], in0=tab, scalar=live[("ss", i)][:, 3:4], in1=y3[:, :, lo:hi],
-                        op0=ALU.mult, op1=ALU.mult,
-                    )
+        def multiply_by_tables(t):
+            frame, parity = divmod(t, 2)
+            cos_part = work.tile([P, HEADS, HEAD], F32, tag="cos_part", name="cos_part")
+            sin_part = work.tile([P, HEADS, HEAD], F32, tag="sin_part", name="sin_part")
+            tiles[("parts", t)] = (cos_part, sin_part)
+            for half in range(2):
+                y_heads = banks[(t, half)].rearrange("p (h d) -> p h d", d=HEAD)
+                heads = slice(4 * half, 4 * half + 4)
+                for cs in range(2):
+                    for lo, hi, table in (
+                        (0, FRAME_PART, frame_table[:, frame, cs, heads, :]),
+                        (FRAME_PART, HEAD, grid_table[:, parity, cs, heads, :]),
+                    ):
+                        nc.vector.scalar_tensor_tensor(
+                            out=tiles[("parts", t)][cs][:, heads, lo:hi], in0=table, scalar=tiles[("stats", t)][:, 3:4],
+                            in1=y_heads[:, :, lo:hi], op0=ALU.mult, op1=ALU.mult,
+                        )
 
-        def add_part(i, hs, cols, eng):
-            if ("o", i) not in live:
-                live[("o", i)] = work.tile([P, K], F32, tag="o", name="o", bufs=3)
-            t1, t2 = live[("t", i)]
-            eng_of(eng).tensor_tensor(
-                out=live[("o", i)][:, cols].rearrange("p (n e) -> p n e", e=2),
-                in0=t1[:, hs, :].rearrange("p h (j e) -> p (h j) e", e=2),
-                in1=t2[:, hs, :].rearrange("p h (j e) -> p (h j) e", e=2)[:, :, ::-1],
+        def add_and_store(t, engine, heads):
+            if ("out", t) not in tiles:
+                tiles[("out", t)] = work.tile([P, FEATURES], F32, tag="rotated", name="rotated", bufs=3)
+            cos_part, sin_part = tiles[("parts", t)]
+            columns = slice(HEAD * heads.start, HEAD * heads.stop)
+            engine.tensor_tensor(
+                out=tiles[("out", t)][:, columns].rearrange("p (n e) -> p n e", e=2),
+                in0=cos_part[:, heads, :].rearrange("p h (j e) -> p (h j) e", e=2),
+                in1=sin_part[:, heads, :].rearrange("p h (j e) -> p (h j) e", e=2)[:, :, ::-1],
                 op=ALU.add,
             )
+            nc.sync.dma_start(out=out_rows[P * t : P * (t + 1), columns], in_=tiles[("out", t)][:, columns])
 
-        def op_add(i):
-            add_part(int(i), slice(0, NH), slice(0, K), "G")
+        def finish(t):
+            multiply_by_tables(t)
+            if t < FIRST_SHARED_ADD:
+                add_and_store(t, nc.gpsimd, slice(0, HEADS))
+            else:
+                add_and_store(t, nc.gpsimd, slice(0, 4))
+                add_and_store(t, nc.vector, slice(4, HEADS))
 
-        def op_st(i):
-            i = int(i)
-            nc.sync.dma_start(out=out_rows[P * i : P * (i + 1), :], in_=live[("o", i)][:])
+        idle_matmuls()
+        spread_gain(0)
+        spread_gain(1)
+        prepare_selection()
+        bring_in("x0", "c0")
+        spread_frame_positions(0)
+        spread_frame_positions(1)
+        pick_grid_positions_and_bias()
+        for frame in range(GPSIMD_FRAME_TABLES):
+            build_frame_table(nc.gpsimd, frame)
+        bring_in("x1", "c1")
+        bring_in("x2", "c0")
+        bring_in("w0", "b0")
+        idle_matmuls()
+        bring_in("x3", "c1")
+        bring_in("w1", "b1")
+        bring_in("w2", "c0")
+        idle_matmuls()
+        bring_in("w3", "c1")
+        quantize_x(0, 0)
+        quantize_x(0, 1)
+        for head in range(4):
+            quantize_w(head)
+        bring_in("w4", "b0")
+        bring_in("w5", "b1")
+        idle_matmuls()
+        bring_in("w6", "c0")
+        bring_in("w7", "c1")
+        for head in range(4, HEADS):
+            quantize_w(head)
+        build_grid_table(0)
+        build_grid_table(1)
+        for frame in range(GPSIMD_FRAME_TABLES, FRAMES):
+            build_frame_table(nc.vector, frame)
 
-        def op_addh(i, bk, eng):
-            bk = int(bk)
-            add_part(int(i), slice(4 * bk, 4 * bk + 4), slice(512 * bk, 512 * (bk + 1)), eng)
+        project(0, 0)
+        project(0, 1)
+        bring_in("x4", "b0")
+        bring_in("x5", "b1")
+        bring_in("x6", "c0")
+        bring_in("x7", "c1")
+        quantize_x(1, 0)
+        quantize_x(1, 1)
+        project(0, 2)
+        project(0, 3)
+        bring_in("x8", "c0")
+        project(0, 4)
+        project(0, 5)
+        turn_back(0, 0)
+        turn_back(1, 0)
+        bring_in("x9", "c1")
+        bring_in("x10", "c0")
+        project(0, 6)
+        project(0, 7)
+        bring_in("x11", "c1")
+        quantize_x(2, 0)
+        quantize_x(2, 1)
+        bring_in("x12", "c0")
+        turn_back(0, 1)
+        turn_back(1, 1)
+        add_eps(0)
+        bring_in("x13", "c1")
+        bring_in("x14", "c0")
+        take_rstd(0)
+        add_eps(1)
+        project(1, 0)
+        take_rstd(1)
+        project(1, 1)
+        bring_in("x15", "c1")
+        finish(0)
+        project(1, 2)
+        project(1, 3)
+        finish(1)
 
-        def op_sth(i, bk):
-            i, bk = int(i), int(bk)
-            cols = slice(512 * bk, 512 * (bk + 1))
-            nc.sync.dma_start(out=out_rows[P * i : P * (i + 1), cols], in_=live[("o", i)][:, cols])
-
-        ops = {
-            "dummy": op_dummy, "gain": op_gain, "gainS": op_gainS, "vec": op_vec, "posT": op_posT, "posTS": op_posTS, "posRC": op_posRC,
-            "posRCS": op_posRCS, "tabT": op_tabT, "tabRC": op_tabRC, "t": op_t, "c": op_c, "qx": op_qx, "qw": op_qw,
-            "mx": op_mx, "sa": op_sa, "bt": op_bt, "sq": op_sq, "tiny1": op_tiny1, "tiny2": op_tiny2, "stt": op_stt,
-            "add": op_add, "st": op_st, "addh": op_addh, "sth": op_sth,
-        }
-        for tok in ORDER:
-            parts = tok.split(" ")
-            ops[parts[0]](*parts[1:])
+        for t in range(2, TILES):
+            chunk, place = divmod(t, 4)
+            turn_back(t, 1)
+            turn_back(t, 0)
+            add_eps(t)
+            if chunk + 1 < CHUNKS:
+                project(chunk + 1, 2 * place)
+            take_rstd(t)
+            if chunk + 1 < CHUNKS:
+                project(chunk + 1, 2 * place + 1)
+            finish(t)
+            if t in (2, 3):
+                quantize_x(3, t - 2)

@@ -30,7 +30,6 @@ EPS = 1e-6
 
 VECTOR_COPIES = ("x0", "x2", "w0", "w2", "w4", "w6", "x9", "x13")
 GPSIMD_FRAME_TABLES = 5
-FIRST_SHARED_ADD = 14
 
 
 def tile_causalwanselfattention_pa_kernel(tc, x, W, b, g, freqs_cos, freqs_sin, out):
@@ -292,10 +291,10 @@ def tile_causalwanselfattention_pa_kernel(tc, x, W, b, g, freqs_cos, freqs_sin, 
 
         def finish(t):
             multiply_by_tables(t)
-            if t < FIRST_SHARED_ADD:
+            if t < TILES - 1:
                 add_and_store(t, nc.gpsimd, slice(0, HEADS))
             else:
-                add_and_store(t, nc.gpsimd, slice(0, 4))
+                add_and_store(t, nc.vector, slice(0, 4))
                 add_and_store(t, nc.vector, slice(4, HEADS))
 
         idle_matmuls()

@@ -39,7 +39,7 @@ def tile_causalwanselfattention_pa_kernel(tc, x, W, b, g, freqs_cos, freqs_sin, 
 
     with ExitStack() as ctx:
         const = ctx.enter_context(tc.tile_pool(name="const", bufs=1))
-        inputs = ctx.enter_context(tc.tile_pool(name="inputs", bufs=24))
+        inputs = ctx.enter_context(tc.tile_pool(name="inputs", bufs=20))
         grouped = ctx.enter_context(tc.tile_pool(name="grouped", bufs=2))
         ypool = ctx.enter_context(tc.tile_pool(name="ypool", bufs=2))
         work = ctx.enter_context(tc.tile_pool(name="work", bufs=4))
@@ -194,23 +194,26 @@ def tile_causalwanselfattention_pa_kernel(tc, x, W, b, g, freqs_cos, freqs_sin, 
                     tiles[("x", chunk)] = grouped.tile([P, PASSES, 4 * CHUNK], BF16, tag="xg", name="xg", align_bytes=64)
                 dst = tiles[("x", chunk)].bitcast(F32)[:, :, 256 * place : 256 * (place + 1)]
             else:
-                tiles[("w", n)] = grouped.tile([P, PASSES, 4 * HEAD], BF16, tag="wg", name="wg", align_bytes=64, bufs=4)
-                dst = tiles[("w", n)].bitcast(F32)
+                if n % 4 == 0:
+                    tiles[("w", n // 4)] = grouped.tile([P, 4, PASSES, 4 * HEAD], BF16, tag="wg", name="wg", align_bytes=64)
+                dst = tiles[("w", n // 4)][:, n % 4].bitcast(F32)
             empty_bank(
                 name in VECTOR_COPIES, dst.rearrange("p g (r u) -> p g r u", u=2), turned.rearrange("p g u r -> p g r u")
             )
 
-        def quantize_x(chunk, gi):
+        def quantize_x(chunk):
             nc.vector.quantize_mx(
-                out=x_codes[:, chunk, gi, :].bitcast(FP8X4), scales=x_scales[:, chunk, gi, :],
-                in_=tiles[("x", chunk)][:, gi, :],
+                out=x_codes[:, chunk].rearrange("p g n -> p (g n)").bitcast(FP8X4),
+                scales=x_scales[:, chunk].rearrange("p g n -> p (g n)"),
+                in_=tiles[("x", chunk)].rearrange("p g n -> p (g n)"),
             )
 
-        def quantize_w(head):
+        def quantize_w(half):
+            heads = slice(4 * half, 4 * half + 4)
             nc.vector.quantize_mx(
-                out=w_codes[:, head].rearrange("p g m -> p (g m)").bitcast(FP8X4),
-                scales=w_scales[:, head].rearrange("p g m -> p (g m)"),
-                in_=tiles[("w", head)].rearrange("p g n -> p (g n)"),
+                out=w_codes[:, heads].rearrange("p h g m -> p (h g m)").bitcast(FP8X4),
+                scales=w_scales[:, heads].rearrange("p h g m -> p (h g m)"),
+                in_=tiles[("w", half)].rearrange("p h g n -> p (h g n)"),
             )
 
         def project(chunk, head):
@@ -298,6 +301,7 @@ def tile_causalwanselfattention_pa_kernel(tc, x, W, b, g, freqs_cos, freqs_sin, 
                 add_and_store(t, nc.vector, slice(4, HEADS))
 
         idle_matmuls()
+        idle_matmuls()
         spread_gain(0)
         spread_gain(1)
         prepare_selection()
@@ -316,17 +320,14 @@ def tile_causalwanselfattention_pa_kernel(tc, x, W, b, g, freqs_cos, freqs_sin, 
         bring_in("w2", "c0")
         idle_matmuls()
         bring_in("w3", "c1")
-        quantize_x(0, 0)
-        quantize_x(0, 1)
-        for head in range(4):
-            quantize_w(head)
+        quantize_x(0)
+        quantize_w(0)
         bring_in("w4", "b0")
         bring_in("w5", "b1")
         idle_matmuls()
         bring_in("w6", "c0")
         bring_in("w7", "c1")
-        for head in range(4, HEADS):
-            quantize_w(head)
+        quantize_w(1)
         build_grid_table(0)
         build_grid_table(1)
         for frame in range(GPSIMD_FRAME_TABLES, FRAMES):
@@ -338,8 +339,7 @@ def tile_causalwanselfattention_pa_kernel(tc, x, W, b, g, freqs_cos, freqs_sin, 
         bring_in("x5", "b1")
         bring_in("x6", "c0")
         bring_in("x7", "c1")
-        quantize_x(1, 0)
-        quantize_x(1, 1)
+        quantize_x(1)
         project(0, 2)
         project(0, 3)
         bring_in("x8", "c0")
@@ -352,19 +352,18 @@ def tile_causalwanselfattention_pa_kernel(tc, x, W, b, g, freqs_cos, freqs_sin, 
         project(0, 6)
         project(0, 7)
         bring_in("x11", "c1")
-        quantize_x(2, 0)
-        quantize_x(2, 1)
+        quantize_x(2)
         bring_in("x12", "c0")
+        project(1, 0)
         turn_back(0, 1)
         turn_back(1, 1)
         add_eps(0)
         bring_in("x13", "c1")
-        bring_in("x14", "c0")
         take_rstd(0)
         add_eps(1)
-        project(1, 0)
-        take_rstd(1)
         project(1, 1)
+        take_rstd(1)
+        bring_in("x14", "c0")
         bring_in("x15", "c1")
         finish(0)
         project(1, 2)
@@ -382,5 +381,5 @@ def tile_causalwanselfattention_pa_kernel(tc, x, W, b, g, freqs_cos, freqs_sin, 
             if chunk + 1 < CHUNKS:
                 project(chunk + 1, 2 * place + 1)
             finish(t)
-            if t in (2, 3):
-                quantize_x(3, t - 2)
+            if t == 2:
+                quantize_x(3)

@@ -28,7 +28,7 @@ GRID_PART = HEAD - FRAME_PART
 ROW_PART = 42
 EPS = 1e-6
 
-VECTOR_COPIES = ("x0", "x2", "w0", "w2", "w4", "w6", "x9", "x13")
+VECTOR_COPIES = ("x0", "x2", "w0", "x9", "x10", "x12", "x13")
 GPSIMD_FRAME_TABLES = 5
 
 
@@ -163,14 +163,23 @@ def tile_causalwanselfattention_pa_kernel(tc, x, W, b, g, freqs_cos, freqs_sin, 
             nc.scalar.copy(out=bias[:], in_=picked[:, width : width + HEADS])
             nc.scalar.copy(out=grid_pos.rearrange("p a c n -> p (a c n)"), in_=picked[:, 0:width])
 
-        def build_frame_table(engine, frame):
+        def build_frame_table_on_vector(frame):
             shape = [P, 2, HEADS, FRAME_PART]
-            engine.tensor_tensor(
+            nc.vector.tensor_tensor(
                 out=frame_table[:, frame],
                 in0=gain_heads[:, :, 0:FRAME_PART].unsqueeze(1).to_broadcast(shape),
                 in1=frame_pos[:, :, frame, :].unsqueeze(2).to_broadcast(shape),
                 op=ALU.mult,
             )
+
+        def build_frame_table_on_gpsimd(frame):
+            for cs in range(2):
+                nc.gpsimd.tensor_tensor(
+                    out=frame_table[:, frame, cs],
+                    in0=gain_heads[:, :, 0:FRAME_PART],
+                    in1=frame_pos[:, cs, frame, :].unsqueeze(1).to_broadcast([P, HEADS, FRAME_PART]),
+                    op=ALU.mult,
+                )
 
         def build_grid_table(parity):
             shape = [P, 2, HEADS, GRID_PART]
@@ -310,7 +319,7 @@ def tile_causalwanselfattention_pa_kernel(tc, x, W, b, g, freqs_cos, freqs_sin, 
         spread_frame_positions(1)
         pick_grid_positions_and_bias()
         for frame in range(GPSIMD_FRAME_TABLES):
-            build_frame_table(nc.gpsimd, frame)
+            build_frame_table_on_gpsimd(frame)
         bring_in("x1", "c1")
         bring_in("x2", "c0")
         bring_in("w0", "b0")
@@ -331,7 +340,7 @@ def tile_causalwanselfattention_pa_kernel(tc, x, W, b, g, freqs_cos, freqs_sin, 
         build_grid_table(0)
         build_grid_table(1)
         for frame in range(GPSIMD_FRAME_TABLES, FRAMES):
-            build_frame_table(nc.vector, frame)
+            build_frame_table_on_vector(frame)
 
         project(0, 0)
         project(0, 1)

@@ -303,11 +303,14 @@ def tile_causalwanselfattention_pa_kernel(tc, x, W, b, g, freqs_cos, freqs_sin, 
 
         def finish(t):
             multiply_by_tables(t)
-            if t < TILES - 1:
+            if t < TILES - 2:
                 add_and_store(t, nc.gpsimd, slice(0, HEADS))
+            elif t == TILES - 2:
+                add_and_store(t, nc.gpsimd, slice(0, 4))
+                add_and_store(t, nc.gpsimd, slice(4, HEADS))
             else:
-                add_and_store(t, nc.vector, slice(0, 4))
-                add_and_store(t, nc.vector, slice(4, HEADS))
+                for first in range(0, HEADS, 2):
+                    add_and_store(t, nc.vector, slice(first, first + 2))
 
         idle_matmuls()
         idle_matmuls()

@@ -30,6 +30,10 @@ EPS = 1e-6
 
 VECTOR_COPIES = ("x0", "x2", "w0", "x9", "x10", "x12", "x13")
 GPSIMD_FRAME_TABLES = 5
+TURNED_HEADS = 6
+TURNED_FRAMES = 2
+TURNED_TILES = 2 * TURNED_FRAMES
+TURNED_WIDTH = 64
 
 
 def tile_causalwanselfattention_pa_kernel(tc, x, W, b, g, freqs_cos, freqs_sin, out):
@@ -48,7 +52,7 @@ def tile_causalwanselfattention_pa_kernel(tc, x, W, b, g, freqs_cos, freqs_sin, 
         ctx.enter_context(tc.manual_schedule())
 
         rows = const.tile([P, 384], BF16, name="rows")
-        nc.vector.memset(rows[:], 0.0)
+        nc.gpsimd.memset(rows.bitcast(F32)[:], 0.0)
         one = const.tile([P, 2], F32, name="one")
         nc.vector.memset(one[:], 1.0)
         ones = const.tile([P, P], BF16, name="ones")
@@ -82,7 +86,12 @@ def tile_causalwanselfattention_pa_kernel(tc, x, W, b, g, freqs_cos, freqs_sin, 
         bias = const.tile([P, HEADS], F32, name="bias")
         frame_pos = const.tile([P, 2, FRAMES, FRAME_PART], F32, name="frame_pos")
         grid_pos = const.tile([P, 2, 2, GRID_PART], F32, name="grid_pos")
-        frame_table = const.tile([P, FRAMES, 2, HEADS, FRAME_PART], F32, name="frame_table")
+        frame_table = const.tile([P, FRAMES - TURNED_FRAMES, 2, HEADS, FRAME_PART], F32, name="frame_table")
+        late_frame_table = const.tile([P, TURNED_FRAMES, 2, HEADS - TURNED_HEADS, FRAME_PART], F32, name="late_frame_table")
+        gain_columns = const.tile([P, HEADS], F32, name="gain_columns")
+        turned_pos = const.tile([P, 2, TURNED_FRAMES, FRAME_PART], F32, name="turned_pos")
+        rotation = const.tile([P, TURNED_FRAMES, FRAME_PART], F32, name="rotation")
+        gained_rotation = const.tile([P, TURNED_HEADS + 1, TURNED_FRAMES, FRAME_PART], F32, name="gained_rotation")
         grid_table = const.tile([P, 2, 2, HEADS, GRID_PART], F32, name="grid_table")
         freq = const.tile([P, 2, HEAD], BF16, name="freq")
         freq_by_frame = const.tile([P, 2, FRAMES, FRAME_PART], BF16, name="freq_by_frame")
@@ -99,7 +108,7 @@ def tile_causalwanselfattention_pa_kernel(tc, x, W, b, g, freqs_cos, freqs_sin, 
                 nc.scalar.copy(out=dst, in_=src)
 
         def idle_matmuls():
-            for bank in ("a0", "a1"):
+            for bank in ("mx0", "mx1"):
                 unused = psum.tile([P, CHUNK], F32, tag=bank, name="unused")
                 nc.tensor.matmul(out=unused[:], lhsT=ones[:], rhs=ones_wide[:], start=True, stop=True)
 
@@ -160,7 +169,12 @@ def tile_causalwanselfattention_pa_kernel(tc, x, W, b, g, freqs_cos, freqs_sin, 
             nc.tensor.matmul(
                 out=picked[:, width : width + HEADS], lhsT=rows[:, 128:256], rhs=ident_bf[:, 0:HEADS], start=True, stop=True
             )
+            nc.tensor.matmul(
+                out=picked[:, width + HEADS : width + 2 * HEADS], lhsT=rows[:, 256:384], rhs=ident_bf[:, 0:HEADS],
+                start=True, stop=True,
+            )
             nc.scalar.copy(out=bias[:], in_=picked[:, width : width + HEADS])
+            nc.scalar.copy(out=gain_columns[:], in_=picked[:, width + HEADS : width + 2 * HEADS])
             nc.scalar.copy(out=grid_pos.rearrange("p a c n -> p (a c n)"), in_=picked[:, 0:width])
 
         def build_frame_table_on_vector(frame):
@@ -171,6 +185,58 @@ def tile_causalwanselfattention_pa_kernel(tc, x, W, b, g, freqs_cos, freqs_sin, 
                 in1=frame_pos[:, :, frame, :].unsqueeze(2).to_broadcast(shape),
                 op=ALU.mult,
             )
+
+        def build_late_frame_tables():
+            shape = [P, TURNED_FRAMES, 2, (HEADS - TURNED_HEADS) * FRAME_PART]
+            for f in range(TURNED_FRAMES):
+                shape = [P, 2, HEADS - TURNED_HEADS, FRAME_PART]
+                nc.vector.tensor_tensor(
+                    out=late_frame_table[:, f],
+                    in0=gain_heads[:, TURNED_HEADS:, 0:FRAME_PART].unsqueeze(1).to_broadcast(shape),
+                    in1=frame_pos[:, :, FRAMES - TURNED_FRAMES + f, :].unsqueeze(2).to_broadcast(shape),
+                    op=ALU.mult,
+                )
+
+        def build_rotations():
+            first = FRAMES - TURNED_FRAMES
+            shape = [P, 2, TURNED_FRAMES, FRAME_PART]
+            nc.gpsimd.tensor_tensor(
+                out=turned_pos[:], in0=ident[:, 0:FRAME_PART].unsqueeze(1).unsqueeze(1).to_broadcast(shape),
+                in1=frame_pos[:, :, first:, :], op=ALU.mult,
+            )
+            nc.gpsimd.tensor_tensor(
+                out=rotation.rearrange("p f (j e) -> p (f j) e", e=2),
+                in0=turned_pos[:, 0].rearrange("p f (j e) -> p (f j) e", e=2),
+                in1=turned_pos[:, 1].rearrange("p f (j e) -> p (f j) e", e=2)[:, :, ::-1],
+                op=ALU.add,
+            )
+            shape = [P, TURNED_HEADS + 1, TURNED_FRAMES * FRAME_PART]
+            nc.gpsimd.tensor_tensor(
+                out=gained_rotation.rearrange("p h f n -> p h (f n)"),
+                in0=rotation.rearrange("p f n -> p (f n)").unsqueeze(1).to_broadcast(shape),
+                in1=gain_columns[:, 0 : TURNED_HEADS + 1].unsqueeze(2).to_broadcast(shape),
+                op=ALU.mult,
+            )
+
+        def rotate_frame_part(t):
+            chunk, place = divmod(t, 4)
+            turned = psum.tile([P, TURNED_HEADS, TURNED_WIDTH], F32, tag="mx%d" % ((t + 1) % 2), name="turned")
+            columns = gained_rotation.rearrange("p h f n -> p (h f n)")
+            for h in range(TURNED_HEADS):
+                first = (TURNED_FRAMES * h + t // 2 - FRAMES + TURNED_FRAMES) * FRAME_PART
+                nc.tensor.matmul(
+                    out=turned[:, h, :], lhsT=tiles[("y", chunk)][:, h, P * place : P * (place + 1)],
+                    rhs=columns[:, first : first + TURNED_WIDTH], start=True, stop=True,
+                )
+            banks[("frame", t)] = turned
+
+        def finish_frame_part(t):
+            nc.scalar.activation(
+                out=tiles[("out", t)].rearrange("p (h d) -> p h d", d=HEAD)[:, 0:TURNED_HEADS, 0:FRAME_PART],
+                in_=banks[("frame", t)][:, :, 0:FRAME_PART], func=ACT.Copy, scale=tiles[("stats", t)][:, 3:4],
+            )
+            columns = slice(0, HEAD * TURNED_HEADS)
+            nc.sync.dma_start(out=out_rows[P * t : P * (t + 1), columns], in_=tiles[("out", t)][:, columns])
 
         def build_frame_table_on_gpsimd(frame):
             for cs in range(2):
@@ -279,14 +345,30 @@ def tile_causalwanselfattention_pa_kernel(tc, x, W, b, g, freqs_cos, freqs_sin, 
                 y_heads = banks[(t, half)].rearrange("p (h d) -> p h d", d=HEAD)
                 heads = slice(4 * half, 4 * half + 4)
                 for cs in range(2):
-                    for lo, hi, table in (
-                        (0, FRAME_PART, frame_table[:, frame, cs, heads, :]),
-                        (FRAME_PART, HEAD, grid_table[:, parity, cs, heads, :]),
-                    ):
+                    parts = [(heads, FRAME_PART, HEAD, grid_table[:, parity, cs, heads, :])]
+                    if t < TILES - TURNED_TILES:
+                        parts.append((heads, 0, FRAME_PART, frame_table[:, frame, cs, heads, :]))
+                    else:
+                        first = max(heads.start, TURNED_HEADS)
+                        late = late_frame_table[:, frame - FRAMES + TURNED_FRAMES, cs, first - TURNED_HEADS : heads.stop - TURNED_HEADS]
+                        if first < heads.stop:
+                            parts.append((slice(first, heads.stop), 0, FRAME_PART, late))
+                    for some, lo, hi, table in parts:
                         nc.vector.scalar_tensor_tensor(
-                            out=tiles[("parts", t)][cs][:, heads, lo:hi], in0=table, scalar=tiles[("stats", t)][:, 3:4],
-                            in1=y_heads[:, :, lo:hi], op0=ALU.mult, op1=ALU.mult,
+                            out=tiles[("parts", t)][cs][:, some, lo:hi], in0=table, scalar=tiles[("stats", t)][:, 3:4],
+                            in1=y_heads[:, some.start - heads.start :, lo:hi], op0=ALU.mult, op1=ALU.mult,
                         )
+
+        def add_grid_part(t, engine, heads):
+            cos_part, sin_part = tiles[("parts", t)]
+            tiles[("out", t)] = work.tile([P, FEATURES], F32, tag="rotated", name="rotated", bufs=3)
+            rotated = tiles[("out", t)].rearrange("p (h d) -> p h d", d=HEAD)
+            engine.tensor_tensor(
+                out=rotated[:, heads, FRAME_PART:].rearrange("p h (j e) -> p h j e", e=2),
+                in0=cos_part[:, heads, FRAME_PART:].rearrange("p h (j e) -> p h j e", e=2),
+                in1=sin_part[:, heads, FRAME_PART:].rearrange("p h (j e) -> p h j e", e=2)[:, :, :, ::-1],
+                op=ALU.add,
+            )
 
         def add_and_store(t, engine, heads):
             if ("out", t) not in tiles:
@@ -303,13 +385,14 @@ def tile_causalwanselfattention_pa_kernel(tc, x, W, b, g, freqs_cos, freqs_sin, 
 
         def finish(t):
             multiply_by_tables(t)
-            if t < TILES - 2:
+            if t < TILES - TURNED_TILES:
                 add_and_store(t, nc.gpsimd, slice(0, HEADS))
-            elif t == TILES - 2:
-                add_and_store(t, nc.gpsimd, slice(0, 4))
-                add_and_store(t, nc.gpsimd, slice(4, HEADS))
+            elif t < TILES - 1:
+                add_grid_part(t, nc.gpsimd, slice(0, TURNED_HEADS))
+                add_and_store(t, nc.gpsimd, slice(TURNED_HEADS, HEADS))
             else:
-                for first in range(0, HEADS, 2):
+                add_grid_part(t, nc.vector, slice(0, TURNED_HEADS))
+                for first in range(TURNED_HEADS, HEADS, 2):
                     add_and_store(t, nc.vector, slice(first, first + 2))
 
         idle_matmuls()
@@ -323,6 +406,7 @@ def tile_causalwanselfattention_pa_kernel(tc, x, W, b, g, freqs_cos, freqs_sin, 
         pick_grid_positions_and_bias()
         for frame in range(GPSIMD_FRAME_TABLES):
             build_frame_table_on_gpsimd(frame)
+        build_rotations()
         bring_in("x1", "c1")
         bring_in("x2", "c0")
         bring_in("w0", "b0")
@@ -342,8 +426,9 @@ def tile_causalwanselfattention_pa_kernel(tc, x, W, b, g, freqs_cos, freqs_sin, 
         quantize_w(1)
         build_grid_table(0)
         build_grid_table(1)
-        for frame in range(GPSIMD_FRAME_TABLES, FRAMES):
+        for frame in range(GPSIMD_FRAME_TABLES, FRAMES - TURNED_FRAMES):
             build_frame_table_on_vector(frame)
+        build_late_frame_tables()
 
         project(0, 0)
         project(0, 1)
@@ -387,11 +472,20 @@ def tile_causalwanselfattention_pa_kernel(tc, x, W, b, g, freqs_cos, freqs_sin, 
             turn_back(t, 1)
             turn_back(t, 0)
             add_eps(t)
+            if t == TILES - TURNED_TILES:
+                idle_matmuls()
             if chunk + 1 < CHUNKS:
                 project(chunk + 1, 2 * place)
             take_rstd(t)
             if chunk + 1 < CHUNKS:
                 project(chunk + 1, 2 * place + 1)
+            if t > TILES - TURNED_TILES:
+                rotate_frame_part(t - 1)
+                finish_frame_part(t - 1)
+            if t == TILES - 1:
+                rotate_frame_part(t)
             finish(t)
+            if t == TILES - 1:
+                finish_frame_part(t)
             if t == 2:
                 quantize_x(3)

@@ -431,9 +431,9 @@ def tile_causalwanselfattention_pa_kernel(tc, x, W, b, g, freqs_cos, freqs_sin, 
         build_late_frame_tables()
 
         project(0, 0)
-        project(0, 1)
         bring_in("x4", "b0")
         bring_in("x5", "b1")
+        project(0, 1)
         bring_in("x6", "c0")
         bring_in("x7", "c1")
         quantize_x(1)
@@ -441,9 +441,9 @@ def tile_causalwanselfattention_pa_kernel(tc, x, W, b, g, freqs_cos, freqs_sin, 
         project(0, 3)
         bring_in("x8", "c0")
         project(0, 4)
-        project(0, 5)
         turn_back(0, 0)
         turn_back(1, 0)
+        project(0, 5)
         bring_in("x9", "c1")
         bring_in("x10", "c0")
         project(0, 6)

@@ -107,8 +107,8 @@ def tile_causalwanselfattention_pa_kernel(tc, x, W, b, g, freqs_cos, freqs_sin, 
             else:
                 nc.scalar.copy(out=dst, in_=src)
 
-        def idle_matmuls():
-            for bank in ("mx0", "mx1"):
+        def idle_matmuls(banks=("mx0", "mx1")):
+            for bank in banks:
                 unused = psum.tile([P, CHUNK], F32, tag=bank, name="unused")
                 nc.tensor.matmul(out=unused[:], lhsT=ones[:], rhs=ones_wide[:], start=True, stop=True)
 
@@ -469,6 +469,8 @@ def tile_causalwanselfattention_pa_kernel(tc, x, W, b, g, freqs_cos, freqs_sin, 
 
         for t in range(2, TILES):
             chunk, place = divmod(t, 4)
+            if t % 4 == 0:
+                idle_matmuls(["%s%d" % ("abc"[t % 3], half) for half in range(2)])
             turn_back(t, 1)
             turn_back(t, 0)
             add_eps(t)

@@ -77,10 +77,10 @@ def tile_causalwanselfattention_pa_kernel(tc, x, W, b, g, freqs_cos, freqs_sin, 
         make_identity(nc, ident[:])
         nc.scalar.activation(out=one[:, 1:2], in_=one[:, 0:1], func=ACT.Abs_reciprocal_sqrt)
 
-        w_codes = const.tile([P, HEADS, PASSES, HEAD], U32, name="w_codes", align_bytes=64)
-        w_scales = const.tile([P, HEADS, PASSES, HEAD], U8, name="w_scales", align_bytes=64)
-        x_codes = const.tile([P, CHUNKS, PASSES, CHUNK], U32, name="x_codes", align_bytes=64)
-        x_scales = const.tile([P, CHUNKS, PASSES, CHUNK], U8, name="x_scales", align_bytes=64)
+        w_codes = const.tile([P, HEADS, PASSES, HEAD], U32, name="w_codes", align_bytes=256)
+        w_scales = const.tile([P, HEADS, PASSES, HEAD], U8, name="w_scales", align_bytes=256)
+        x_codes = const.tile([P, CHUNKS, PASSES, CHUNK], U32, name="x_codes", align_bytes=256)
+        x_scales = const.tile([P, CHUNKS, PASSES, CHUNK], U8, name="x_scales", align_bytes=256)
         gain = const.tile([P, FEATURES], F32, name="gain")
         gain_heads = gain.rearrange("p (h d) -> p h d", d=HEAD)
         bias = const.tile([P, HEADS], F32, name="bias")
@@ -440,11 +440,11 @@ def tile_causalwanselfattention_pa_kernel(tc, x, W, b, g, freqs_cos, freqs_sin, 
         project(0, 2)
         project(0, 3)
         bring_in("x8", "c0")
+        bring_in("x9", "c1")
         project(0, 4)
+        project(0, 5)
         turn_back(0, 0)
         turn_back(1, 0)
-        project(0, 5)
-        bring_in("x9", "c1")
         bring_in("x10", "c0")
         project(0, 6)
         project(0, 7)

@@ -28,7 +28,7 @@ GRID_PART = HEAD - FRAME_PART
 ROW_PART = 42
 EPS = 1e-6
 
-VECTOR_COPIES = ("x0", "x2", "w0", "x9", "x10", "x12", "x13")
+VECTOR_COPIES = ("x0", "x2", "w0", "x9", "x10", "x11", "x13")
 GPSIMD_FRAME_TABLES = 5
 TURNED_HEADS = 6
 TURNED_FRAMES = 2

@@ -30,7 +30,7 @@ EPS = 1e-6
 
 VECTOR_COPIES = ("x0", "x2", "w0", "x9", "x10", "x11", "x13")
 GPSIMD_FRAME_TABLES = 5
-TURNED_HEADS = 6
+TURNED_HEADS = 7
 TURNED_FRAMES = 2
 TURNED_TILES = 2 * TURNED_FRAMES
 TURNED_WIDTH = 64
@@ -350,8 +350,8 @@ def tile_causalwanselfattention_pa_kernel(tc, x, W, b, g, freqs_cos, freqs_sin, 
                         parts.append((heads, 0, FRAME_PART, frame_table[:, frame, cs, heads, :]))
                     else:
                         first = max(heads.start, TURNED_HEADS)
-                        late = late_frame_table[:, frame - FRAMES + TURNED_FRAMES, cs, first - TURNED_HEADS : heads.stop - TURNED_HEADS]
                         if first < heads.stop:
+                            late = late_frame_table[:, frame - FRAMES + TURNED_FRAMES, cs, first - TURNED_HEADS : heads.stop - TURNED_HEADS]
                             parts.append((slice(first, heads.stop), 0, FRAME_PART, late))
                     for some, lo, hi, table in parts:
                         nc.vector.scalar_tensor_tensor(
@@ -393,9 +393,8 @@ def tile_causalwanselfattention_pa_kernel(tc, x, W, b, g, freqs_cos, freqs_sin, 
             else:
                 add_grid_part(t, nc.vector, slice(0, TURNED_HEADS))
                 for first in range(TURNED_HEADS, HEADS, 2):
-                    add_and_store(t, nc.vector, slice(first, first + 2))
+                    add_and_store(t, nc.vector, slice(first, min(first + 2, HEADS)))
 
-        idle_matmuls()
         idle_matmuls()
         spread_gain(0)
         spread_gain(1)

from contextlib import ExitStack

import concourse.mybir as mybir
from concourse.masks import make_identity

FLOPS = 2 * 2048 * 1024 * 1024

F32 = mybir.dt.float32
BF16 = mybir.dt.bfloat16
U32 = mybir.dt.uint32
U8 = mybir.dt.uint8
FP8X4 = mybir.dt.float8_e5m2_x4
ACT = mybir.ActivationFunctionType
ALU = mybir.AluOpType

P = 128
K = 1024
PASSES = 2
HEADS = 8
HEAD = 128
FEATURES = HEADS * HEAD
CHUNK = 512
CHUNKS = 4
TILES = 16
FRAMES = 8
FRAME_PART = 44
GRID_PART = HEAD - FRAME_PART
ROW_PART = 42
EPS = 1e-6

VECTOR_COPIES = ("x0", "x2", "w0", "x9", "x10", "x11", "x13")
GPSIMD_FRAME_TABLES = 5
TURNED_HEADS = 7
TURNED_FRAMES = 2
TURNED_TILES = 2 * TURNED_FRAMES
TURNED_WIDTH = 64


def tile_causalwanselfattention_pa_kernel(tc, x, W, b, g, freqs_cos, freqs_sin, out):
    nc = tc.nc
    x_rows = x.rearrange("o l k -> (o l) k")
    out_rows = out.rearrange("o l h d -> (o l) (h d)")

    with ExitStack() as ctx:
        const = ctx.enter_context(tc.tile_pool(name="const", bufs=1))
        inputs = ctx.enter_context(tc.tile_pool(name="inputs", bufs=20))
        grouped = ctx.enter_context(tc.tile_pool(name="grouped", bufs=2))
        ypool = ctx.enter_context(tc.tile_pool(name="ypool", bufs=2))
        work = ctx.enter_context(tc.tile_pool(name="work", bufs=4))
        small = ctx.enter_context(tc.tile_pool(name="small", bufs=4))
        psum = ctx.enter_context(tc.psum_pool(name="psum", bufs=1))
        ctx.enter_context(tc.manual_schedule())

        rows = const.tile([P, 384], BF16, name="rows")
        nc.gpsimd.memset(rows.bitcast(F32)[:], 0.0)
        one = const.tile([P, 2], F32, name="one")
        nc.vector.memset(one[:], 1.0)
        ones = const.tile([P, P], BF16, name="ones")
        nc.vector.memset(ones[:], 1.0)
        ones_wide = const.tile([P, CHUNK], BF16, name="ones_wide")
        nc.vector.memset(ones_wide[:], 1.0)
        nc.scalar.dma_start(out=rows[0:16, 0:64], in_=freqs_cos)
        nc.scalar.dma_start(out=rows[0:16, 64:128], in_=freqs_sin)
        nc.sync.dma_start(out=rows[0:HEADS, 256:384], in_=g.rearrange("(h d) -> h d", d=HEAD))
        nc.sync.dma_start(out=rows[0:HEADS, 128:256], in_=b.rearrange("(h d) -> h d", d=HEAD))

        raw = {}
        for name in ["x%d" % t for t in range(4)] + ["w%d" % h for h in range(HEADS)] + ["x%d" % t for t in range(4, TILES)]:
            n = int(name[1:])
            raw[name] = inputs.tile([P, K], BF16, tag="raw", name="raw_" + name)
            source = x_rows if name[0] == "x" else W
            nc.sync.dma_start(out=raw[name][:], in_=source[P * n : P * (n + 1), :])

        ident_bf = const.tile([P, P], BF16, name="ident_bf")
        make_identity(nc, ident_bf[:])
        ident = const.tile([P, P], F32, name="ident")
        make_identity(nc, ident[:])
        nc.scalar.activation(out=one[:, 1:2], in_=one[:, 0:1], func=ACT.Abs_reciprocal_sqrt)

        w_codes = const.tile([P, HEADS, PASSES, HEAD], U32, name="w_codes", align_bytes=256)
        w_scales = const.tile([P, HEADS, PASSES, HEAD], U8, name="w_scales", align_bytes=256)
        x_codes = const.tile([P, CHUNKS, PASSES, CHUNK], U32, name="x_codes", align_bytes=256)
        x_scales = const.tile([P, CHUNKS, PASSES, CHUNK], U8, name="x_scales", align_bytes=256)
        gain = const.tile([P, FEATURES], F32, name="gain")
        gain_heads = gain.rearrange("p (h d) -> p h d", d=HEAD)
        bias = const.tile([P, HEADS], F32, name="bias")
        frame_pos = const.tile([P, 2, FRAMES, FRAME_PART], F32, name="frame_pos")
        grid_pos = const.tile([P, 2, 2, GRID_PART], F32, name="grid_pos")
        frame_table = const.tile([P, FRAMES - TURNED_FRAMES, 2, HEADS, FRAME_PART], F32, name="frame_table")
        late_frame_table = const.tile([P, TURNED_FRAMES, 2, HEADS - TURNED_HEADS, FRAME_PART], F32, name="late_frame_table")
        gain_columns = const.tile([P, HEADS], F32, name="gain_columns")
        turned_pos = const.tile([P, 2, TURNED_FRAMES, FRAME_PART], F32, name="turned_pos")
        rotation = const.tile([P, TURNED_FRAMES, FRAME_PART], F32, name="rotation")
        gained_rotation = const.tile([P, TURNED_HEADS + 1, TURNED_FRAMES, FRAME_PART], F32, name="gained_rotation")
        grid_table = const.tile([P, 2, 2, HEADS, GRID_PART], F32, name="grid_table")
        freq = const.tile([P, 2, HEAD], BF16, name="freq")
        freq_by_frame = const.tile([P, 2, FRAMES, FRAME_PART], BF16, name="freq_by_frame")
        pick_row = const.tile([P, 2, P], BF16, name="pick_row")
        pick_column = const.tile([P, P], BF16, name="pick_column")

        banks = {}
        tiles = {}

        def empty_bank(on_vector, dst, src):
            if on_vector:
                nc.vector.tensor_copy(out=dst, in_=src)
            else:
                nc.scalar.copy(out=dst, in_=src)

        def idle_matmuls(banks=("mx0", "mx1")):
            for bank in banks:
                unused = psum.tile([P, CHUNK], F32, tag=bank, name="unused")
                nc.tensor.matmul(out=unused[:], lhsT=ones[:], rhs=ones_wide[:], start=True, stop=True)

        def spread_gain(half):
            spread = psum.tile([P, CHUNK], F32, tag="a%d" % half, name="spread")
            for i in range(4):
                h = 4 * half + i
                nc.tensor.matmul(
                    out=spread[:, HEAD * i : HEAD * (i + 1)], lhsT=ident_bf[:, h : h + 1].to_broadcast([P, P]),
                    rhs=rows[:, 256:384], start=True, stop=True,
                )
            nc.scalar.copy(out=gain[:, CHUNK * half : CHUNK * (half + 1)], in_=spread[:])

        def prepare_selection():
            nc.vector.tensor_copy(
                out=freq.rearrange("p c (j e) -> p (c j) e", e=2), in_=rows[:, 0:128].unsqueeze(2).to_broadcast([P, P, 2])
            )
            nc.vector.tensor_copy(
                out=pick_row.rearrange("p a (b c) -> p (a b) c", c=16),
                in_=ident_bf[:, 0:16].unsqueeze(2).to_broadcast([P, 16, 16]),
            )
            sin_odd = freq.rearrange("p c (j e) -> p c j e", e=2)[:, 1, :, 1:2]
            nc.vector.tensor_scalar_mul(out=sin_odd, in0=sin_odd, scalar1=-1.0)
            nc.vector.tensor_copy(
                out=pick_column.rearrange("p (a c) -> p a c", c=16),
                in_=ident_bf[:, 0:16].unsqueeze(1).to_broadcast([P, 8, 16]),
            )
            nc.vector.tensor_tensor(
                out=freq_by_frame[:],
                in0=freq[:, :, 0:FRAME_PART].unsqueeze(2).to_broadcast([P, 2, FRAMES, FRAME_PART]),
                in1=ident_bf[:, 0:FRAMES].unsqueeze(1).unsqueeze(3).to_broadcast([P, 2, FRAMES, FRAME_PART]),
                op=ALU.mult,
            )

        def spread_frame_positions(cs):
            spread = psum.tile([P, CHUNK], F32, tag="b%d" % cs, name="spread")
            width = FRAMES * FRAME_PART
            nc.tensor.matmul(
                out=spread[:, 0:width], lhsT=ones[:], rhs=freq_by_frame[:, cs].rearrange("p f d -> p (f d)"),
                start=True, stop=True,
            )
            nc.scalar.copy(out=frame_pos[:, cs].rearrange("p f d -> p (f d)"), in_=spread[:, 0:width])

        def pick_grid_positions_and_bias():
            picked = psum.tile([P, CHUNK], F32, tag="mx0", name="picked")
            for parity in range(2):
                for cs in range(2):
                    at = GRID_PART * (2 * parity + cs)
                    nc.tensor.matmul(
                        out=picked[:, at : at + ROW_PART], lhsT=pick_row[:, parity, :],
                        rhs=freq[:, cs, FRAME_PART : FRAME_PART + ROW_PART], start=True, stop=True,
                    )
                    nc.tensor.matmul(
                        out=picked[:, at + ROW_PART : at + GRID_PART], lhsT=pick_column[:],
                        rhs=freq[:, cs, FRAME_PART + ROW_PART : HEAD], start=True, stop=True,
                    )
            width = 4 * GRID_PART
            nc.tensor.matmul(
                out=picked[:, width : width + HEADS], lhsT=rows[:, 128:256], rhs=ident_bf[:, 0:HEADS], start=True, stop=True
            )
            nc.tensor.matmul(
                out=picked[:, width + HEADS : width + 2 * HEADS], lhsT=rows[:, 256:384], rhs=ident_bf[:, 0:HEADS],
                start=True, stop=True,
            )
            nc.scalar.copy(out=bias[:], in_=picked[:, width : width + HEADS])
            nc.scalar.copy(out=gain_columns[:], in_=picked[:, width + HEADS : width + 2 * HEADS])
            nc.scalar.copy(out=grid_pos.rearrange("p a c n -> p (a c n)"), in_=picked[:, 0:width])

        def build_frame_table_on_vector(frame):
            shape = [P, 2, HEADS, FRAME_PART]
            nc.vector.tensor_tensor(
                out=frame_table[:, frame],
                in0=gain_heads[:, :, 0:FRAME_PART].unsqueeze(1).to_broadcast(shape),
                in1=frame_pos[:, :, frame, :].unsqueeze(2).to_broadcast(shape),
                op=ALU.mult,
            )

        def build_late_frame_tables():
            shape = [P, TURNED_FRAMES, 2, (HEADS - TURNED_HEADS) * FRAME_PART]
            for f in range(TURNED_FRAMES):
                shape = [P, 2, HEADS - TURNED_HEADS, FRAME_PART]
                nc.vector.tensor_tensor(
                    out=late_frame_table[:, f],
                    in0=gain_heads[:, TURNED_HEADS:, 0:FRAME_PART].unsqueeze(1).to_broadcast(shape),
                    in1=frame_pos[:, :, FRAMES - TURNED_FRAMES + f, :].unsqueeze(2).to_broadcast(shape),
                    op=ALU.mult,
                )

        def build_rotations():
            first = FRAMES - TURNED_FRAMES
            shape = [P, 2, TURNED_FRAMES, FRAME_PART]
            nc.gpsimd.tensor_tensor(
                out=turned_pos[:], in0=ident[:, 0:FRAME_PART].unsqueeze(1).unsqueeze(1).to_broadcast(shape),
                in1=frame_pos[:, :, first:, :], op=ALU.mult,
            )
            nc.gpsimd.tensor_tensor(
                out=rotation.rearrange("p f (j e) -> p (f j) e", e=2),
                in0=turned_pos[:, 0].rearrange("p f (j e) -> p (f j) e", e=2),
                in1=turned_pos[:, 1].rearrange("p f (j e) -> p (f j) e", e=2)[:, :, ::-1],
                op=ALU.add,
            )
            shape = [P, TURNED_HEADS + 1, TURNED_FRAMES * FRAME_PART]
            nc.gpsimd.tensor_tensor(
                out=gained_rotation.rearrange("p h f n -> p h (f n)"),
                in0=rotation.rearrange("p f n -> p (f n)").unsqueeze(1).to_broadcast(shape),
                in1=gain_columns[:, 0 : TURNED_HEADS + 1].unsqueeze(2).to_broadcast(shape),
                op=ALU.mult,
            )

        def rotate_frame_part(t):
            chunk, place = divmod(t, 4)
            turned = psum.tile([P, TURNED_HEADS, TURNED_WIDTH], F32, tag="mx%d" % ((t + 1) % 2), name="turned")
            columns = gained_rotation.rearrange("p h f n -> p (h f n)")
            for h in range(TURNED_HEADS):
                first = (TURNED_FRAMES * h + t // 2 - FRAMES + TURNED_FRAMES) * FRAME_PART
                nc.tensor.matmul(
                    out=turned[:, h, :], lhsT=tiles[("y", chunk)][:, h, P * place : P * (place + 1)],
                    rhs=columns[:, first : first + TURNED_WIDTH], start=True, stop=True,
                )
            banks[("frame", t)] = turned

        def finish_frame_part(t):
            nc.scalar.activation(
                out=tiles[("out", t)].rearrange("p (h d) -> p h d", d=HEAD)[:, 0:TURNED_HEADS, 0:FRAME_PART],
                in_=banks[("frame", t)][:, :, 0:FRAME_PART], func=ACT.Copy, scale=tiles[("stats", t)][:, 3:4],
            )
            columns = slice(0, HEAD * TURNED_HEADS)
            nc.sync.dma_start(out=out_rows[P * t : P * (t + 1), columns], in_=tiles[("out", t)][:, columns])

        def build_frame_table_on_gpsimd(frame):
            for cs in range(2):
                nc.gpsimd.tensor_tensor(
                    out=frame_table[:, frame, cs],
                    in0=gain_heads[:, :, 0:FRAME_PART],
                    in1=frame_pos[:, cs, frame, :].unsqueeze(1).to_broadcast([P, HEADS, FRAME_PART]),
                    op=ALU.mult,
                )

        def build_grid_table(parity):
            shape = [P, 2, HEADS, GRID_PART]
            nc.vector.tensor_tensor(
                out=grid_table[:, parity],
                in0=gain_heads[:, :, FRAME_PART:HEAD].unsqueeze(1).to_broadcast(shape),
                in1=grid_pos[:, parity].unsqueeze(2).to_broadcast(shape),
                op=ALU.mult,
            )

        def bring_in(name, bank):
            words = raw[name].bitcast(F32)
            turned = psum.tile([P, PASSES, 2, P], F32, tag=bank, name="turned_" + name)
            for gi in range(PASSES):
                for u in range(2):
                    nc.tensor.transpose(turned[:, gi, u, :], words[:, 256 * gi + u : 256 * (gi + 1) : 2], ident[:])
            n = int(name[1:])
            if name[0] == "x":
                chunk, place = divmod(n, 4)
                if place == 0:
                    tiles[("x", chunk)] = grouped.tile([P, PASSES, 4 * CHUNK], BF16, tag="xg", name="xg", align_bytes=64)
                dst = tiles[("x", chunk)].bitcast(F32)[:, :, 256 * place : 256 * (place + 1)]
            else:
                if n % 4 == 0:
                    tiles[("w", n // 4)] = grouped.tile([P, 4, PASSES, 4 * HEAD], BF16, tag="wg", name="wg", align_bytes=64)
                dst = tiles[("w", n // 4)][:, n % 4].bitcast(F32)
            empty_bank(
                name in VECTOR_COPIES, dst.rearrange("p g (r u) -> p g r u", u=2), turned.rearrange("p g u r -> p g r u")
            )

        def quantize_x(chunk):
            nc.vector.quantize_mx(
                out=x_codes[:, chunk].rearrange("p g n -> p (g n)").bitcast(FP8X4),
                scales=x_scales[:, chunk].rearrange("p g n -> p (g n)"),
                in_=tiles[("x", chunk)].rearrange("p g n -> p (g n)"),
            )

        def quantize_w(half):
            heads = slice(4 * half, 4 * half + 4)
            nc.vector.quantize_mx(
                out=w_codes[:, heads].rearrange("p h g m -> p (h g m)").bitcast(FP8X4),
                scales=w_scales[:, heads].rearrange("p h g m -> p (h g m)"),
                in_=tiles[("w", half)].rearrange("p h g n -> p (h g n)"),
            )

        def project(chunk, head):
            acc = psum.tile([P, CHUNK], F32, tag="mx%d" % ((head + 1) % 2), name="acc")
            for gi in range(PASSES):
                nc.tensor.matmul_mx(
                    out=acc[:],
                    lhsT=w_codes[:, head, gi, :].bitcast(FP8X4),
                    lhsT_scale=w_scales[:, head, gi, :],
                    rhs=x_codes[:, chunk, gi, :].bitcast(FP8X4),
                    rhs_scale=x_scales[:, chunk, gi, :],
                    start=(gi == 0),
                    stop=(gi == PASSES - 1),
                )
            if head == 0:
                tiles[("y", chunk)] = ypool.tile([P, HEADS, CHUNK], F32, tag="y", name="y")
            nc.scalar.activation(
                out=tiles[("y", chunk)][:, head, :], in_=acc[:], func=ACT.Identity, bias=bias[:, head : head + 1], scale=1.0
            )

        def turn_back(t, half):
            chunk, place = divmod(t, 4)
            y_tokens = psum.tile([P, CHUNK], F32, tag="%s%d" % ("abc"[t % 3], half), name="y_tokens")
            for i in range(4):
                nc.tensor.transpose(
                    y_tokens[:, HEAD * i : HEAD * (i + 1)],
                    tiles[("y", chunk)][:, 4 * half + i, P * place : P * (place + 1)], ident[:],
                )
            banks[(t, half)] = y_tokens
            if ("stats", t) not in tiles:
                tiles[("stats", t)] = small.tile([P, 4], F32, tag="stats", name="stats")
            squares = work.tile([P, CHUNK], F32, tag="squares", name="squares", bufs=2)
            nc.scalar.activation(
                out=squares[:], in_=y_tokens[:], func=ACT.Square, scale=0.03125,
                accum_out=tiles[("stats", t)][:, half : half + 1],
            )

        def add_eps(t):
            stats = tiles[("stats", t)]
            nc.scalar.activation(out=stats[:, 2:3], in_=stats[:, 1:2], func=ACT.Identity, bias=EPS, scale=1.0)

        def take_rstd(t):
            stats = tiles[("stats", t)]
            nc.scalar.activation(
                out=stats[:, 3:4], in_=stats[:, 0:1], func=ACT.Abs_reciprocal_sqrt, bias=stats[:, 2:3], scale=1.0
            )

        def multiply_by_tables(t):
            frame, parity = divmod(t, 2)
            cos_part = work.tile([P, HEADS, HEAD], F32, tag="cos_part", name="cos_part")
            sin_part = work.tile([P, HEADS, HEAD], F32, tag="sin_part", name="sin_part")
            tiles[("parts", t)] = (cos_part, sin_part)
            for half in range(2):
                y_heads = banks[(t, half)].rearrange("p (h d) -> p h d", d=HEAD)
                heads = slice(4 * half, 4 * half + 4)
                for cs in range(2):
                    parts = [(heads, FRAME_PART, HEAD, grid_table[:, parity, cs, heads, :])]
                    if t < TILES - TURNED_TILES:
                        parts.append((heads, 0, FRAME_PART, frame_table[:, frame, cs, heads, :]))
                    else:
                        first = max(heads.start, TURNED_HEADS)
                        if first < heads.stop:
                            late = late_frame_table[:, frame - FRAMES + TURNED_FRAMES, cs, first - TURNED_HEADS : heads.stop - TURNED_HEADS]
                            parts.append((slice(first, heads.stop), 0, FRAME_PART, late))
                    for some, lo, hi, table in parts:
                        nc.vector.scalar_tensor_tensor(
                            out=tiles[("parts", t)][cs][:, some, lo:hi], in0=table, scalar=tiles[("stats", t)][:, 3:4],
                            in1=y_heads[:, some.start - heads.start :, lo:hi], op0=ALU.mult, op1=ALU.mult,
                        )

        def add_grid_part(t, engine, heads):
            cos_part, sin_part = tiles[("parts", t)]
            tiles[("out", t)] = work.tile([P, FEATURES], F32, tag="rotated", name="rotated", bufs=3)
            rotated = tiles[("out", t)].rearrange("p (h d) -> p h d", d=HEAD)
            engine.tensor_tensor(
                out=rotated[:, heads, FRAME_PART:].rearrange("p h (j e) -> p h j e", e=2),
                in0=cos_part[:, heads, FRAME_PART:].rearrange("p h (j e) -> p h j e", e=2),
                in1=sin_part[:, heads, FRAME_PART:].rearrange("p h (j e) -> p h j e", e=2)[:, :, :, ::-1],
                op=ALU.add,
            )

        def add_and_store(t, engine, heads):
            if ("out", t) not in tiles:
                tiles[("out", t)] = work.tile([P, FEATURES], F32, tag="rotated", name="rotated", bufs=3)
            cos_part, sin_part = tiles[("parts", t)]
            columns = slice(HEAD * heads.start, HEAD * heads.stop)
            engine.tensor_tensor(
                out=tiles[("out", t)][:, columns].rearrange("p (n e) -> p n e", e=2),
                in0=cos_part[:, heads, :].rearrange("p h (j e) -> p (h j) e", e=2),
                in1=sin_part[:, heads, :].rearrange("p h (j e) -> p (h j) e", e=2)[:, :, ::-1],
                op=ALU.add,
            )
            nc.sync.dma_start(out=out_rows[P * t : P * (t + 1), columns], in_=tiles[("out", t)][:, columns])

        def finish(t):
            multiply_by_tables(t)
            if t < TILES - TURNED_TILES:
                add_and_store(t, nc.gpsimd, slice(0, HEADS))
            elif t < TILES - 1:
                add_grid_part(t, nc.gpsimd, slice(0, TURNED_HEADS))
                add_and_store(t, nc.gpsimd, slice(TURNED_HEADS, HEADS))
            else:
                add_grid_part(t, nc.vector, slice(0, TURNED_HEADS))
                for first in range(TURNED_HEADS, HEADS, 2):
                    add_and_store(t, nc.vector, slice(first, min(first + 2, HEADS)))

        idle_matmuls()
        spread_gain(0)
        spread_gain(1)
        prepare_selection()
        bring_in("x0", "c0")
        spread_frame_positions(0)
        spread_frame_positions(1)
        pick_grid_positions_and_bias()
        for frame in range(GPSIMD_FRAME_TABLES):
            build_frame_table_on_gpsimd(frame)
        build_rotations()
        bring_in("x1", "c1")
        bring_in("x2", "c0")
        bring_in("w0", "b0")
        idle_matmuls()
        bring_in("x3", "c1")
        bring_in("w1", "b1")
        bring_in("w2", "c0")
        idle_matmuls()
        bring_in("w3", "c1")
        quantize_x(0)
        quantize_w(0)
        bring_in("w4", "b0")
        bring_in("w5", "b1")
        idle_matmuls()
        bring_in("w6", "c0")
        bring_in("w7", "c1")
        quantize_w(1)
        build_grid_table(0)
        build_grid_table(1)
        for frame in range(GPSIMD_FRAME_TABLES, FRAMES - TURNED_FRAMES):
            build_frame_table_on_vector(frame)
        build_late_frame_tables()

        project(0, 0)
        bring_in("x4", "b0")
        bring_in("x5", "b1")
        project(0, 1)
        bring_in("x6", "c0")
        bring_in("x7", "c1")
        quantize_x(1)
        project(0, 2)
        project(0, 3)
        bring_in("x8", "c0")
        bring_in("x9", "c1")
        project(0, 4)
        project(0, 5)
        turn_back(0, 0)
        turn_back(1, 0)
        bring_in("x10", "c0")
        project(0, 6)
        project(0, 7)
        bring_in("x11", "c1")
        quantize_x(2)
        bring_in("x12", "c0")
        project(1, 0)
        turn_back(0, 1)
        turn_back(1, 1)
        add_eps(0)
        bring_in("x13", "c1")
        take_rstd(0)
        add_eps(1)
        project(1, 1)
        take_rstd(1)
        bring_in("x14", "c0")
        bring_in("x15", "c1")
        finish(0)
        project(1, 2)
        project(1, 3)
        finish(1)

        for t in range(2, TILES):
            chunk, place = divmod(t, 4)
            if t % 4 == 0:
                idle_matmuls(["%s%d" % ("abc"[t % 3], half) for half in range(2)])
            turn_back(t, 1)
            turn_back(t, 0)
            add_eps(t)
            if t == TILES - TURNED_TILES:
                idle_matmuls()
            if chunk + 1 < CHUNKS:
                project(chunk + 1, 2 * place)
            take_rstd(t)
            if chunk + 1 < CHUNKS:
                project(chunk + 1, 2 * place + 1)
            if t > TILES - TURNED_TILES:
                rotate_frame_part(t - 1)
                finish_frame_part(t - 1)
            if t == TILES - 1:
                rotate_frame_part(t)
            finish(t)
            if t == TILES - 1:
                finish_frame_part(t)
            if t == 2:
                quantize_x(3)
